import numpy as np
import ml_dtypes


def mxq(x, axis, fmt="e4m3"):
    dtype, down = {"e4m3": (ml_dtypes.float8_e4m3fn, 7), "e5m2": (ml_dtypes.float8_e5m2, 14)}[fmt]
    v = np.moveaxis(np.asarray(x, np.float32).astype(ml_dtypes.bfloat16).astype(np.float64), axis, -1)
    blocks = v.reshape(v.shape[:-1] + (-1, 32))
    amax = np.abs(blocks).max(-1, keepdims=True)
    byte = np.maximum(np.where(amax > 0, np.frexp(amax)[1] - 1 + 127, 0) - down, 1)
    scale = np.exp2(byte - 127.0)
    codes = (blocks / scale).astype(np.float32).astype(dtype).astype(np.float64)
    return np.moveaxis((codes * scale).reshape(v.shape), -1, axis)


WIDE = False


def mx_kscale(k):
    if not WIDE:
        return np.ones(k)
    levels = np.array([10, -10, 5, -5, 0])
    a = np.random.permutation(np.resize(levels, k // 512 * 4)).reshape(k // 512, 4)
    idx = np.arange(k)
    return np.exp2(a[idx // 512, idx % 128 // 32])


BF16 = ml_dtypes.bfloat16


def bf(x):
    return np.asarray(x, np.float32).astype(BF16)


def f64(x):
    return np.asarray(x).astype(np.float64)


B, S, D_IN, D_OUT = 2, 64, 1024, 1024


def setup_inputs():
    s = mx_kscale(D_IN)
    m = s.min()
    return {"x": bf(np.random.standard_normal((B, S, D_IN)) * s),
            "weight": bf(np.random.standard_normal((D_OUT, D_IN)) * 0.9 / np.sqrt(D_IN) * (m / s) ** 2),
            "alpha": bf((1.0 + 0.1 * np.random.standard_normal(1)) * 1.3 / np.sqrt(D_IN) / m),
            "bias": bf(np.random.standard_normal(D_OUT) * 0.1)}


def reference(x, weight, alpha, bias):
    w = f64(weight)
    delta = 0.7 * np.mean(np.abs(w))
    w_t = np.where(w > delta, 1.0, np.where(w < -delta, -1.0, 0.0))
    w_q = w_t * f64(alpha)
    return (mxq(f64(x), 2, "e4m3") @ mxq(w_q, 1, "e4m3").T) + f64(bias)

@@ -1,0 +1,166 @@
+from contextlib import ExitStack
+
+import concourse.mybir as mybir
+from concourse.masks import make_identity
+
+BF16 = mybir.dt.bfloat16
+F32 = mybir.dt.float32
+I32 = mybir.dt.int32
+U32 = mybir.dt.uint32
+U8 = mybir.dt.uint8
+FP8X4 = mybir.dt.float8_e4m3fn_x4
+ALU = mybir.AluOpType
+ACT = mybir.ActivationFunctionType
+
+P = 128
+D_IN = 1024
+D_OUT = 1024
+O_TILES = D_OUT // P
+K_PASS = 4 * P
+PASSES = D_IN // K_PASS
+WORDS = D_IN // 2
+TURNS = WORDS // P
+CODE_COLS = PASSES * P
+MAGNITUDE_BITS = 0x7FFF7FFF
+SUM_COLS = 16
+
+FLOPS = 2 * P * D_IN * D_OUT
+
+
+def turn_and_group(nc, psum, rows_bf16, ident, grouped):
+    words = rows_bf16.bitcast(F32)
+    turned = psum.tile([P, TURNS, P], F32, tag="turned")
+    for j in range(TURNS):
+        nc.tensor.transpose(turned[:, j, :], words[:, j * P : (j + 1) * P], ident)
+    nc.scalar.copy(
+        out=grouped.bitcast(F32).rearrange("p (g r u) -> p g r u", g=PASSES, u=2),
+        in_=turned[:].rearrange("p (g u) r -> p g r u", u=2),
+    )
+
+
+def tile_ternarylinear_s_kernel(tc, x, weight, alpha, bias, out):
+    nc = tc.nc
+    x_rows = x.flatten_outer_dims()
+    out_rows = out.flatten_outer_dims()
+    w_tiles = weight.rearrange("(t p) d -> t p d", p=P)
+
+    with ExitStack() as ctx:
+        keep = ctx.enter_context(tc.tile_pool(name="keep", bufs=1))
+        work = ctx.enter_context(tc.tile_pool(name="work", bufs=3))
+        every = ctx.enter_context(tc.tile_pool(name="every", bufs=O_TILES))
+        psum_turn = ctx.enter_context(tc.psum_pool(name="psum_turn", bufs=3))
+        psum_out = ctx.enter_context(tc.psum_pool(name="psum_out", bufs=4))
+        psum_sum = ctx.enter_context(tc.psum_pool(name="psum_sum", bufs=1))
+
+        ident = keep.tile([P, P], F32)
+        make_identity(nc, ident[:])
+        mean_weights = keep.tile([P, P], F32)
+        nc.vector.memset(mean_weights[:], 0.7 / (D_OUT * D_IN))
+        partial = keep.tile([P, SUM_COLS], F32)
+        nc.vector.memset(partial[:], 0.0)
+
+        alpha_bf = keep.tile([P, 1], BF16)
+        nc.scalar.dma_start(out=alpha_bf[:], in_=alpha.partition_broadcast(P))
+        w_sb = keep.tile([P, O_TILES, D_IN], BF16)
+        for t in range(O_TILES):
+            nc.sync.dma_start(out=w_sb[:, t, :], in_=w_tiles[t])
+        x_sb = keep.tile([P, D_IN], BF16)
+        nc.sync.dma_start(out=x_sb[:], in_=x_rows)
+        bias_sb = keep.tile([P, D_OUT], BF16)
+        nc.sync.dma_start(out=bias_sb[:], in_=bias.partition_broadcast(P))
+
+        magnitude = keep.tile([P, O_TILES, D_IN], BF16)
+        half_sign = keep.tile([P, O_TILES, D_IN], BF16)
+        for t in range(O_TILES):
+            if t % 2 == 0:
+                nc.scalar.activation(
+                    out=magnitude[:, t, :],
+                    in_=w_sb[:, t, :],
+                    func=ACT.Abs,
+                    accum_out=partial[:, t // 2 : t // 2 + 1],
+                )
+            else:
+                nc.vector.tensor_scalar(
+                    out=magnitude[:, t, :].bitcast(I32),
+                    in0=w_sb[:, t, :].bitcast(I32),
+                    scalar1=MAGNITUDE_BITS,
+                    scalar2=None,
+                    op0=ALU.bitwise_and,
+                )
+                unused = work.tile([P, D_IN], BF16)
+                nc.vector.tensor_scalar(
+                    out=unused[:],
+                    in0=magnitude[:, t, :],
+                    scalar1=1.0,
+                    scalar2=None,
+                    op0=ALU.mult,
+                    op1=ALU.add,
+                    accum_out=partial[:, 8 + t // 2 : 8 + t // 2 + 1],
+                )
+            nc.vector.tensor_scalar(
+                out=half_sign[:, t, :],
+                in0=w_sb[:, t, :],
+                scalar1=0.0,
+                scalar2=0.5,
+                op0=ALU.is_ge,
+                op1=ALU.subtract,
+            )
+
+        total = psum_sum.tile([P, SUM_COLS], F32)
+        nc.tensor.matmul(out=total[:], lhsT=mean_weights[:], rhs=partial[:], start=True, stop=True)
+        delta = keep.tile([P, 1], F32)
+        nc.vector.tensor_reduce(out=delta[:], in_=total[:], axis=mybir.AxisListType.X, op=ALU.add)
+        twice_alpha = keep.tile([P, 1], F32)
+        nc.vector.tensor_scalar(
+            out=twice_alpha[:], in0=alpha_bf[:], scalar1=2.0, scalar2=None, op0=ALU.mult
+        )
+
+        x_grouped = keep.tile([P, D_IN], BF16, align_bytes=64)
+        turn_and_group(nc, psum_turn, x_sb[:], ident[:], x_grouped[:])
+        x_codes = keep.tile([P, CODE_COLS], U32, align_bytes=64)
+        x_scales = keep.tile([P, CODE_COLS], U8, align_bytes=64)
+        nc.vector.quantize_mx(out=x_codes[:].bitcast(FP8X4), scales=x_scales[:], in_=x_grouped[:])
+
+        w_grouped = []
+        for t in range(O_TILES):
+            kept = work.tile([P, D_IN], BF16)
+            nc.vector.tensor_scalar(
+                out=kept[:],
+                in0=magnitude[:, t, :],
+                scalar1=delta[:, 0:1],
+                scalar2=twice_alpha[:, 0:1],
+                op0=ALU.is_gt,
+                op1=ALU.mult,
+            )
+            w_q = work.tile([P, D_IN], BF16)
+            nc.vector.tensor_tensor(out=w_q[:], in0=kept[:], in1=half_sign[:, t, :], op=ALU.mult)
+            grouped = every.tile([P, D_IN], BF16, align_bytes=64)
+            turn_and_group(nc, psum_turn, w_q[:], ident[:], grouped[:])
+            w_grouped.append(grouped)
+
+        out_sb = keep.tile([P, D_OUT], F32)
+        for t in range(O_TILES):
+            w_codes = work.tile([P, CODE_COLS], U32, align_bytes=64)
+            w_scales = work.tile([P, CODE_COLS], U8, align_bytes=64)
+            nc.vector.quantize_mx(
+                out=w_codes[:].bitcast(FP8X4), scales=w_scales[:], in_=w_grouped[t][:]
+            )
+            acc = psum_out.tile([P, P], F32)
+            for g in range(PASSES):
+                cols = slice(g * P, (g + 1) * P)
+                nc.tensor.matmul_mx(
+                    out=acc[:],
+                    lhsT=x_codes[:, cols].bitcast(FP8X4),
+                    lhsT_scale=x_scales[:, cols],
+                    rhs=w_codes[:, cols].bitcast(FP8X4),
+                    rhs_scale=w_scales[:, cols],
+                    start=(g == 0),
+                    stop=(g == PASSES - 1),
+                )
+            o_cols = slice(t * P, (t + 1) * P)
+            nc.vector.tensor_tensor(
+                out=out_sb[:, o_cols], in0=acc[:], in1=bias_sb[:, o_cols], op=ALU.add
+            )
+            if t % 2 == 1:
+                pair = slice((t - 1) * P, (t + 1) * P)
+                nc.sync.dma_start(out=out_rows[:, pair], in_=out_sb[:, pair])

@@ -21,6 +21,8 @@ PASSES = D_IN // K_PASS
 WORDS = D_IN // 2
 TURNS = WORDS // P
 CODE_COLS = PASSES * P
+BANK_COLS = 512
+STORE_COLS = 256
 MAGNITUDE_BITS = 0x7FFF7FFF
 SUM_COLS = 16
 
@@ -45,11 +47,12 @@ def tile_ternarylinear_s_kernel(tc, x, weight, alpha, bias, out):
     w_tiles = weight.rearrange("(t p) d -> t p d", p=P)
 
     with ExitStack() as ctx:
+        ctx.enter_context(tc.manual_schedule())
         keep = ctx.enter_context(tc.tile_pool(name="keep", bufs=1))
         work = ctx.enter_context(tc.tile_pool(name="work", bufs=3))
         every = ctx.enter_context(tc.tile_pool(name="every", bufs=O_TILES))
-        psum_turn = ctx.enter_context(tc.psum_pool(name="psum_turn", bufs=3))
-        psum_out = ctx.enter_context(tc.psum_pool(name="psum_out", bufs=4))
+        psum_turn = ctx.enter_context(tc.psum_pool(name="psum_turn", bufs=4))
+        psum_out = ctx.enter_context(tc.psum_pool(name="psum_out", bufs=D_OUT // BANK_COLS))
         psum_sum = ctx.enter_context(tc.psum_pool(name="psum_sum", bufs=1))
 
         ident = keep.tile([P, P], F32)
@@ -57,7 +60,16 @@ def tile_ternarylinear_s_kernel(tc, x, weight, alpha, bias, out):
         mean_weights = keep.tile([P, P], F32)
         nc.vector.memset(mean_weights[:], 0.7 / (D_OUT * D_IN))
         partial = keep.tile([P, SUM_COLS], F32)
-        nc.vector.memset(partial[:], 0.0)
+        delta = psum_sum.tile([P, 1], F32)
+
+        def add_to_delta(col, first=False, last=False):
+            nc.tensor.matmul(
+                out=delta[:],
+                lhsT=mean_weights[:],
+                rhs=partial[:, col : col + 1],
+                start=first,
+                stop=last,
+            )
 
         alpha_bf = keep.tile([P, 1], BF16)
         nc.scalar.dma_start(out=alpha_bf[:], in_=alpha.partition_broadcast(P))
@@ -71,32 +83,8 @@ def tile_ternarylinear_s_kernel(tc, x, weight, alpha, bias, out):
 
         magnitude = keep.tile([P, O_TILES, D_IN], BF16)
         half_sign = keep.tile([P, O_TILES, D_IN], BF16)
-        for t in range(O_TILES):
-            if t % 2 == 0:
-                nc.scalar.activation(
-                    out=magnitude[:, t, :],
-                    in_=w_sb[:, t, :],
-                    func=ACT.Abs,
-                    accum_out=partial[:, t // 2 : t // 2 + 1],
-                )
-            else:
-                nc.vector.tensor_scalar(
-                    out=magnitude[:, t, :].bitcast(I32),
-                    in0=w_sb[:, t, :].bitcast(I32),
-                    scalar1=MAGNITUDE_BITS,
-                    scalar2=None,
-                    op0=ALU.bitwise_and,
-                )
-                unused = work.tile([P, D_IN], BF16)
-                nc.vector.tensor_scalar(
-                    out=unused[:],
-                    in0=magnitude[:, t, :],
-                    scalar1=1.0,
-                    scalar2=None,
-                    op0=ALU.mult,
-                    op1=ALU.add,
-                    accum_out=partial[:, 8 + t // 2 : 8 + t // 2 + 1],
-                )
+
+        def sign_of(t):
             nc.vector.tensor_scalar(
                 out=half_sign[:, t, :],
                 in0=w_sb[:, t, :],
@@ -106,10 +94,38 @@ def tile_ternarylinear_s_kernel(tc, x, weight, alpha, bias, out):
                 op1=ALU.subtract,
             )
 
-        total = psum_sum.tile([P, SUM_COLS], F32)
-        nc.tensor.matmul(out=total[:], lhsT=mean_weights[:], rhs=partial[:], start=True, stop=True)
-        delta = keep.tile([P, 1], F32)
-        nc.vector.tensor_reduce(out=delta[:], in_=total[:], axis=mybir.AxisListType.X, op=ALU.add)
+        sign_of(0)
+        for i in range(O_TILES // 2):
+            even = 2 * i
+            odd = even + 1
+            nc.scalar.activation(
+                out=magnitude[:, even, :],
+                in_=w_sb[:, even, :],
+                func=ACT.Abs,
+                accum_out=partial[:, i : i + 1],
+            )
+            add_to_delta(i, first=(i == 0))
+            nc.vector.tensor_scalar(
+                out=magnitude[:, odd, :].bitcast(I32),
+                in0=w_sb[:, odd, :].bitcast(I32),
+                scalar1=MAGNITUDE_BITS,
+                scalar2=None,
+                op0=ALU.bitwise_and,
+            )
+            sign_of(i + 1)
+            unused = work.tile([P, D_IN], BF16)
+            nc.vector.tensor_scalar(
+                out=unused[:],
+                in0=magnitude[:, odd, :],
+                scalar1=1.0,
+                scalar2=None,
+                op0=ALU.mult,
+                op1=ALU.add,
+                accum_out=partial[:, 8 + i : 8 + i + 1],
+            )
+            add_to_delta(8 + i, last=(odd == O_TILES - 1))
+        for t in range(O_TILES // 2 + 1, O_TILES):
+            sign_of(t)
         twice_alpha = keep.tile([P, 1], F32)
         nc.vector.tensor_scalar(
             out=twice_alpha[:], in0=alpha_bf[:], scalar1=2.0, scalar2=None, op0=ALU.mult
@@ -117,13 +133,9 @@ def tile_ternarylinear_s_kernel(tc, x, weight, alpha, bias, out):
 
         x_grouped = keep.tile([P, D_IN], BF16, align_bytes=64)
         turn_and_group(nc, psum_turn, x_sb[:], ident[:], x_grouped[:])
-        x_codes = keep.tile([P, CODE_COLS], U32, align_bytes=64)
-        x_scales = keep.tile([P, CODE_COLS], U8, align_bytes=64)
-        nc.vector.quantize_mx(out=x_codes[:].bitcast(FP8X4), scales=x_scales[:], in_=x_grouped[:])
 
-        w_grouped = []
-        for t in range(O_TILES):
-            kept = work.tile([P, D_IN], BF16)
+        def keep_large(t):
+            kept = work.tile([P, D_IN], BF16, tag="kept")
             nc.vector.tensor_scalar(
                 out=kept[:],
                 in0=magnitude[:, t, :],
@@ -132,24 +144,40 @@ def tile_ternarylinear_s_kernel(tc, x, weight, alpha, bias, out):
                 op0=ALU.is_gt,
                 op1=ALU.mult,
             )
+            return kept
+
+        w_grouped = []
+        kept_next = keep_large(0)
+        for t in range(O_TILES):
+            kept_now = kept_next
+            if t + 1 < O_TILES:
+                kept_next = keep_large(t + 1)
             w_q = work.tile([P, D_IN], BF16)
-            nc.vector.tensor_tensor(out=w_q[:], in0=kept[:], in1=half_sign[:, t, :], op=ALU.mult)
+            nc.vector.tensor_tensor(
+                out=w_q[:], in0=kept_now[:], in1=half_sign[:, t, :], op=ALU.mult
+            )
             grouped = every.tile([P, D_IN], BF16, align_bytes=64)
             turn_and_group(nc, psum_turn, w_q[:], ident[:], grouped[:])
             w_grouped.append(grouped)
 
-        out_sb = keep.tile([P, D_OUT], F32)
+        x_codes = keep.tile([P, CODE_COLS], U32, align_bytes=64)
+        x_scales = keep.tile([P, CODE_COLS], U8, align_bytes=64)
+        nc.vector.quantize_mx(out=x_codes[:].bitcast(FP8X4), scales=x_scales[:], in_=x_grouped[:])
+        acc_banks = []
         for t in range(O_TILES):
             w_codes = work.tile([P, CODE_COLS], U32, align_bytes=64)
             w_scales = work.tile([P, CODE_COLS], U8, align_bytes=64)
             nc.vector.quantize_mx(
                 out=w_codes[:].bitcast(FP8X4), scales=w_scales[:], in_=w_grouped[t][:]
             )
-            acc = psum_out.tile([P, P], F32)
+            first_col = (t * P) % BANK_COLS
+            if first_col == 0:
+                acc = psum_out.tile([P, BANK_COLS], F32)
+                acc_banks.append(acc)
             for g in range(PASSES):
                 cols = slice(g * P, (g + 1) * P)
                 nc.tensor.matmul_mx(
-                    out=acc[:],
+                    out=acc_banks[-1][:, first_col : first_col + P],
                     lhsT=x_codes[:, cols].bitcast(FP8X4),
                     lhsT_scale=x_scales[:, cols],
                     rhs=w_codes[:, cols].bitcast(FP8X4),
@@ -157,10 +185,15 @@ def tile_ternarylinear_s_kernel(tc, x, weight, alpha, bias, out):
                     start=(g == 0),
                     stop=(g == PASSES - 1),
                 )
-            o_cols = slice(t * P, (t + 1) * P)
+
+        out_sb = keep.tile([P, D_OUT], F32)
+        for first_col in range(0, D_OUT, STORE_COLS):
+            o_cols = slice(first_col, first_col + STORE_COLS)
+            in_bank = first_col % BANK_COLS
             nc.vector.tensor_tensor(
-                out=out_sb[:, o_cols], in0=acc[:], in1=bias_sb[:, o_cols], op=ALU.add
+                out=out_sb[:, o_cols],
+                in0=acc_banks[first_col // BANK_COLS][:, in_bank : in_bank + STORE_COLS],
+                in1=bias_sb[:, o_cols],
+                op=ALU.add,
             )
-            if t % 2 == 1:
-                pair = slice((t - 1) * P, (t + 1) * P)
-                nc.sync.dma_start(out=out_rows[:, pair], in_=out_sb[:, pair])
+            nc.sync.dma_start(out=out_rows[:, o_cols], in_=out_sb[:, o_cols])

@@ -25,6 +25,11 @@ BANK_COLS = 512
 STORE_COLS = 256
 MAGNITUDE_BITS = 0x7FFF7FFF
 SUM_COLS = 16
+SCALAR_TILES = (0, 2, 4)
+TENSOR_TILES = (1, 3, 5)
+SHARED_TILE = 6
+VECTOR_COLS = 384
+LAST_TILE = 7
 
 FLOPS = 2 * P * D_IN * D_OUT
 
@@ -60,11 +65,14 @@ def tile_ternarylinear_s_kernel(tc, x, weight, alpha, bias, out):
         mean_weights = keep.tile([P, P], F32)
         nc.vector.memset(mean_weights[:], 0.7 / (D_OUT * D_IN))
         partial = keep.tile([P, SUM_COLS], F32)
-        delta = psum_sum.tile([P, 1], F32)
+        delta = psum_sum.tile([P, BANK_COLS], F32, tag="delta")
+        col_sums = psum_sum.tile([P, BANK_COLS], F32, tag="col_sums")
+        ones = keep.tile([P, 1], BF16)
+        nc.vector.memset(ones[:], 1.0)
 
         def add_to_delta(col, first=False, last=False):
             nc.tensor.matmul(
-                out=delta[:],
+                out=delta[:, 0:1],
                 lhsT=mean_weights[:],
                 rhs=partial[:, col : col + 1],
                 start=first,
@@ -94,38 +102,66 @@ def tile_ternarylinear_s_kernel(tc, x, weight, alpha, bias, out):
                 op1=ALU.subtract,
             )
 
-        sign_of(0)
-        for i in range(O_TILES // 2):
-            even = 2 * i
-            odd = even + 1
-            nc.scalar.activation(
-                out=magnitude[:, even, :],
-                in_=w_sb[:, even, :],
-                func=ACT.Abs,
-                accum_out=partial[:, i : i + 1],
-            )
-            add_to_delta(i, first=(i == 0))
+        def abs_on_vector(t, cols):
             nc.vector.tensor_scalar(
-                out=magnitude[:, odd, :].bitcast(I32),
-                in0=w_sb[:, odd, :].bitcast(I32),
+                out=magnitude[:, t, cols].bitcast(I32),
+                in0=w_sb[:, t, cols].bitcast(I32),
                 scalar1=MAGNITUDE_BITS,
                 scalar2=None,
                 op0=ALU.bitwise_and,
             )
-            sign_of(i + 1)
-            unused = work.tile([P, D_IN], BF16)
+
+        def abs_and_sum_on_scalar(t, cols, sum_col):
+            nc.scalar.activation(
+                out=magnitude[:, t, cols],
+                in_=w_sb[:, t, cols],
+                func=ACT.Abs,
+                accum_out=partial[:, sum_col : sum_col + 1],
+            )
+
+        def sum_on_vector(t, cols, sum_col):
+            unused = work.tile([P, D_IN], BF16, tag="unused")
             nc.vector.tensor_scalar(
-                out=unused[:],
-                in0=magnitude[:, odd, :],
+                out=unused[:, cols],
+                in0=magnitude[:, t, cols],
                 scalar1=1.0,
                 scalar2=None,
                 op0=ALU.mult,
                 op1=ALU.add,
-                accum_out=partial[:, 8 + i : 8 + i + 1],
+                accum_out=partial[:, sum_col : sum_col + 1],
             )
-            add_to_delta(8 + i, last=(odd == O_TILES - 1))
-        for t in range(O_TILES // 2 + 1, O_TILES):
-            sign_of(t)
+
+        whole = slice(0, D_IN)
+        vector_cols = slice(0, VECTOR_COLS)
+        scalar_cols = slice(VECTOR_COLS, D_IN)
+        sign_of(0)
+        for i in range(3):
+            abs_and_sum_on_scalar(SCALAR_TILES[i], whole, i)
+            t = TENSOR_TILES[i]
+            abs_on_vector(t, whole)
+            for j in range(D_IN // P):
+                nc.tensor.matmul(
+                    out=col_sums[:, 0:1],
+                    lhsT=magnitude[:, t, j * P : (j + 1) * P],
+                    rhs=ones[:],
+                    start=(i == 0 and j == 0),
+                    stop=(i == 2 and j == D_IN // P - 1),
+                )
+            if i < 2:
+                sign_of(t)
+                sign_of(t + 1)
+        abs_and_sum_on_scalar(SHARED_TILE, scalar_cols, 3)
+        abs_on_vector(SHARED_TILE, vector_cols)
+        sign_of(5)
+        sum_on_vector(SHARED_TILE, vector_cols, 5)
+        nc.vector.tensor_copy(out=partial[:, 4:5], in_=col_sums[:, 0:1])
+        abs_on_vector(LAST_TILE, whole)
+        nc.vector.reduce_sum(out=partial[:, 7:8], in_=partial[:, 0:6], axis=mybir.AxisListType.X)
+        sum_on_vector(LAST_TILE, whole, 6)
+        add_to_delta(7, first=True)
+        add_to_delta(6, last=True)
+        sign_of(6)
+        sign_of(7)
         twice_alpha = keep.tile([P, 1], F32)
         nc.vector.tensor_scalar(
             out=twice_alpha[:], in0=alpha_bf[:], scalar1=2.0, scalar2=None, op0=ALU.mult

@@ -79,13 +79,13 @@ def tile_ternarylinear_s_kernel(tc, x, weight, alpha, bias, out):
                 stop=last,
             )
 
-        alpha_bf = keep.tile([P, 1], BF16)
-        nc.scalar.dma_start(out=alpha_bf[:], in_=alpha.partition_broadcast(P))
         w_sb = keep.tile([P, O_TILES, D_IN], BF16)
         for t in range(O_TILES):
             nc.sync.dma_start(out=w_sb[:, t, :], in_=w_tiles[t])
         x_sb = keep.tile([P, D_IN], BF16)
         nc.sync.dma_start(out=x_sb[:], in_=x_rows)
+        alpha_bf = keep.tile([P, 1], BF16)
+        nc.sync.dma_start(out=alpha_bf[:], in_=alpha.partition_broadcast(P))
         bias_sb = keep.tile([P, D_OUT], BF16)
         nc.sync.dma_start(out=bias_sb[:], in_=bias.partition_broadcast(P))
 

@@ -22,9 +22,11 @@ WORDS = D_IN // 2
 TURNS = WORDS // P
 CODE_COLS = PASSES * P
 BANK_COLS = 512
-STORE_COLS = 256
+STORES = (256, 256, 256, 128, 128)
 MAGNITUDE_BITS = 0x7FFF7FFF
+STEEP = 2.0**100
 SUM_COLS = 16
+EARLY_TILES = (0, 1, 2)
 SCALAR_TILES = (0, 2, 4)
 TENSOR_TILES = (1, 3, 5)
 SHARED_TILE = 6
@@ -34,15 +36,30 @@ LAST_TILE = 7
 FLOPS = 2 * P * D_IN * D_OUT
 
 
-def turn_and_group(nc, psum, rows_bf16, ident, grouped):
+def turn(nc, psum, rows_bf16, ident):
     words = rows_bf16.bitcast(F32)
     turned = psum.tile([P, TURNS, P], F32, tag="turned")
     for j in range(TURNS):
         nc.tensor.transpose(turned[:, j, :], words[:, j * P : (j + 1) * P], ident)
+    return turned
+
+
+def copy_grouped(nc, turned, grouped):
     nc.scalar.copy(
         out=grouped.bitcast(F32).rearrange("p (g r u) -> p g r u", g=PASSES, u=2),
         in_=turned[:].rearrange("p (g u) r -> p g r u", u=2),
     )
+
+
+def turn_in_order(nc, psum, rows_bf16, ident):
+    words = rows_bf16.bitcast(F32)
+    turned = psum.tile([P, WORDS], F32, tag="turned")
+    by_word = turned[:].rearrange("p (g r u) -> p g r u", g=PASSES, u=2)
+    for g in range(PASSES):
+        for u in range(2):
+            j = 2 * g + u
+            nc.tensor.transpose(by_word[:, g, :, u], words[:, j * P : (j + 1) * P], ident)
+    return turned
 
 
 def tile_ternarylinear_s_kernel(tc, x, weight, alpha, bias, out):
@@ -55,7 +72,6 @@ def tile_ternarylinear_s_kernel(tc, x, weight, alpha, bias, out):
         ctx.enter_context(tc.manual_schedule())
         keep = ctx.enter_context(tc.tile_pool(name="keep", bufs=1))
         work = ctx.enter_context(tc.tile_pool(name="work", bufs=3))
-        every = ctx.enter_context(tc.tile_pool(name="every", bufs=O_TILES))
         psum_turn = ctx.enter_context(tc.psum_pool(name="psum_turn", bufs=4))
         psum_out = ctx.enter_context(tc.psum_pool(name="psum_out", bufs=D_OUT // BANK_COLS))
         psum_sum = ctx.enter_context(tc.psum_pool(name="psum_sum", bufs=1))
@@ -69,6 +85,8 @@ def tile_ternarylinear_s_kernel(tc, x, weight, alpha, bias, out):
         col_sums = psum_sum.tile([P, BANK_COLS], F32, tag="col_sums")
         ones = keep.tile([P, 1], BF16)
         nc.vector.memset(ones[:], 1.0)
+        table_loader = keep.tile([P, 1], BF16)
+        nc.scalar.activation(out=table_loader[:], in_=ones[:], func=ACT.Sigmoid)
 
         def add_to_delta(col, first=False, last=False):
             nc.tensor.matmul(
@@ -119,13 +137,13 @@ def tile_ternarylinear_s_kernel(tc, x, weight, alpha, bias, out):
                 accum_out=partial[:, sum_col : sum_col + 1],
             )
 
-        def sum_on_vector(t, cols, sum_col):
+        def sum_on_vector(t, cols, sum_col, initial=None):
             unused = work.tile([P, D_IN], BF16, tag="unused")
             nc.vector.tensor_scalar(
                 out=unused[:, cols],
                 in0=magnitude[:, t, cols],
                 scalar1=1.0,
-                scalar2=None,
+                scalar2=initial,
                 op0=ALU.mult,
                 op1=ALU.add,
                 accum_out=partial[:, sum_col : sum_col + 1],
@@ -134,102 +152,192 @@ def tile_ternarylinear_s_kernel(tc, x, weight, alpha, bias, out):
         whole = slice(0, D_IN)
         vector_cols = slice(0, VECTOR_COLS)
         scalar_cols = slice(VECTOR_COLS, D_IN)
-        sign_of(0)
-        for i in range(3):
-            abs_and_sum_on_scalar(SCALAR_TILES[i], whole, i)
-            t = TENSOR_TILES[i]
-            abs_on_vector(t, whole)
+        def sum_on_tensor(t, first=False, last=False):
             for j in range(D_IN // P):
                 nc.tensor.matmul(
                     out=col_sums[:, 0:1],
                     lhsT=magnitude[:, t, j * P : (j + 1) * P],
                     rhs=ones[:],
-                    start=(i == 0 and j == 0),
-                    stop=(i == 2 and j == D_IN // P - 1),
+                    start=(first and j == 0),
+                    stop=(last and j == D_IN // P - 1),
                 )
-            if i < 2:
-                sign_of(t)
-                sign_of(t + 1)
+
+        early_sign = keep.tile([P, len(EARLY_TILES), D_IN], BF16, align_bytes=64)
+        early_alpha = keep.tile([P, len(EARLY_TILES), D_IN], BF16, align_bytes=64)
+        x_grouped = keep.tile([P, D_IN], BF16, align_bytes=64)
+        turned_sign = {}
+
+        def turn_sign(t):
+            turned_sign[t] = turn(nc, psum_turn, half_sign[:, t, :], ident[:])
+
+        for i in range(3):
+            abs_and_sum_on_scalar(SCALAR_TILES[i], whole, i)
         abs_and_sum_on_scalar(SHARED_TILE, scalar_cols, 3)
-        abs_on_vector(SHARED_TILE, vector_cols)
+
+        sign_of(0)
+        turn_sign(0)
+        abs_on_vector(1, whole)
+        sum_on_tensor(1, first=True)
+        sign_of(1)
+        turn_sign(1)
+        sign_of(2)
+        abs_on_vector(3, whole)
+        sum_on_tensor(3)
+        turn_sign(2)
+        sign_of(3)
+        sign_of(4)
+        abs_on_vector(5, whole)
+        sum_on_tensor(5, last=True)
         sign_of(5)
+        abs_on_vector(SHARED_TILE, vector_cols)
+        sign_of(6)
         sum_on_vector(SHARED_TILE, vector_cols, 5)
         nc.vector.tensor_copy(out=partial[:, 4:5], in_=col_sums[:, 0:1])
         abs_on_vector(LAST_TILE, whole)
         nc.vector.reduce_sum(out=partial[:, 7:8], in_=partial[:, 0:6], axis=mybir.AxisListType.X)
-        sum_on_vector(LAST_TILE, whole, 6)
-        add_to_delta(7, first=True)
-        add_to_delta(6, last=True)
-        sign_of(6)
         sign_of(7)
+        sum_on_vector(LAST_TILE, whole, 6, initial=partial[:, 7:8])
+        turned_x = turn(nc, psum_turn, x_sb[:], ident[:])
+        copy_grouped(nc, turned_sign[0], early_sign[:, 0, :])
+        copy_grouped(nc, turned_sign[1], early_sign[:, 1, :])
+        copy_grouped(nc, turned_x, x_grouped[:])
+        copy_grouped(nc, turned_sign[2], early_sign[:, 2, :])
+        add_to_delta(6, first=True, last=True)
         twice_alpha = keep.tile([P, 1], F32)
         nc.vector.tensor_scalar(
             out=twice_alpha[:], in0=alpha_bf[:], scalar1=2.0, scalar2=None, op0=ALU.mult
         )
 
-        x_grouped = keep.tile([P, D_IN], BF16, align_bytes=64)
-        turn_and_group(nc, psum_turn, x_sb[:], ident[:], x_grouped[:])
-
-        def keep_large(t):
-            kept = work.tile([P, D_IN], BF16, tag="kept")
+        def sign_to_alpha(t):
             nc.vector.tensor_scalar(
-                out=kept[:],
+                out=early_alpha[:, t, :],
+                in0=early_sign[:, t, :],
+                scalar1=twice_alpha[:, 0:1],
+                scalar2=None,
+                op0=ALU.mult,
+            )
+
+        sign_to_alpha(0)
+        sign_to_alpha(1)
+        x_codes = keep.tile([P, CODE_COLS], U32, align_bytes=64)
+        x_scales = keep.tile([P, CODE_COLS], U8, align_bytes=64)
+        nc.vector.quantize_mx(out=x_codes[:].bitcast(FP8X4), scales=x_scales[:], in_=x_grouped[:])
+        step_bias = keep.tile([P, 1], F32)
+        nc.vector.tensor_scalar(
+            out=step_bias[:],
+            in0=delta[:, 0:1],
+            scalar1=-STEEP * (1.0 + 2.0**-22),
+            scalar2=-1000.0,
+            op0=ALU.mult,
+            op1=ALU.add,
+        )
+
+        w_grouped = keep.tile([P, O_TILES, D_IN], BF16, align_bytes=64)
+        mask_of = {}
+        turned_mask_of = {}
+
+        def mask_on_vector(t):
+            mask = work.tile([P, D_IN], BF16, tag="mask")
+            nc.vector.tensor_scalar(
+                out=mask[:],
                 in0=magnitude[:, t, :],
                 scalar1=delta[:, 0:1],
                 scalar2=twice_alpha[:, 0:1],
                 op0=ALU.is_gt,
                 op1=ALU.mult,
             )
-            return kept
+            mask_of[t] = mask
 
-        w_grouped = []
-        kept_next = keep_large(0)
-        for t in range(O_TILES):
-            kept_now = kept_next
-            if t + 1 < O_TILES:
-                kept_next = keep_large(t + 1)
-            w_q = work.tile([P, D_IN], BF16)
+        def mask_on_scalar(t):
+            mask = work.tile([P, D_IN], BF16, tag="scalar_mask")
+            nc.scalar.activation(
+                out=mask[:],
+                in_=magnitude[:, t, :],
+                func=ACT.Sigmoid,
+                scale=STEEP,
+                bias=step_bias[:, 0:1],
+            )
+            mask_of[t] = mask
+
+        def turn_mask(t):
+            turned_mask_of[t] = turn_in_order(nc, psum_turn, mask_of[t][:], ident[:])
+
+        def product_of_turned(t):
             nc.vector.tensor_tensor(
-                out=w_q[:], in0=kept_now[:], in1=half_sign[:, t, :], op=ALU.mult
+                out=w_grouped[:, t, :],
+                in0=turned_mask_of[t][:].bitcast(BF16),
+                in1=early_alpha[:, t, :],
+                op=ALU.mult,
             )
-            grouped = every.tile([P, D_IN], BF16, align_bytes=64)
-            turn_and_group(nc, psum_turn, w_q[:], ident[:], grouped[:])
-            w_grouped.append(grouped)
 
-        x_codes = keep.tile([P, CODE_COLS], U32, align_bytes=64)
-        x_scales = keep.tile([P, CODE_COLS], U8, align_bytes=64)
-        nc.vector.quantize_mx(out=x_codes[:].bitcast(FP8X4), scales=x_scales[:], in_=x_grouped[:])
-        acc_banks = []
-        for t in range(O_TILES):
-            w_codes = work.tile([P, CODE_COLS], U32, align_bytes=64)
-            w_scales = work.tile([P, CODE_COLS], U8, align_bytes=64)
-            nc.vector.quantize_mx(
-                out=w_codes[:].bitcast(FP8X4), scales=w_scales[:], in_=w_grouped[t][:]
+        def product_then_turn(t):
+            w_q = work.tile([P, D_IN], BF16, tag="w_q")
+            nc.vector.tensor_tensor(
+                out=w_q[:], in0=mask_of[t][:], in1=half_sign[:, t, :], op=ALU.mult
             )
+            copy_grouped(nc, turn(nc, psum_turn, w_q[:], ident[:]), w_grouped[:, t, :])
+
+        mask_on_scalar(0)
+        mask_on_scalar(1)
+        mask_on_vector(3)
+        mask_on_vector(4)
+        product_then_turn(3)
+        turn_mask(0)
+        mask_on_scalar(2)
+        mask_on_vector(5)
+        product_then_turn(4)
+        turn_mask(1)
+        mask_on_vector(6)
+        product_then_turn(5)
+        turn_mask(2)
+        sign_to_alpha(2)
+        product_of_turned(0)
+        mask_on_vector(7)
+        product_of_turned(1)
+        product_then_turn(6)
+        product_then_turn(7)
+        product_of_turned(2)
+
+        w_codes = keep.tile([P, O_TILES, CODE_COLS], U32, align_bytes=64)
+        w_scales = keep.tile([P, O_TILES, CODE_COLS], U8, align_bytes=64)
+        acc_banks = []
+        for i in range(D_OUT // BANK_COLS):
+            acc = psum_out.tile([P, BANK_COLS], F32)
+            acc_banks.append(acc)
+
+        def quantise(t):
+            nc.vector.quantize_mx(
+                out=w_codes[:, t, :].bitcast(FP8X4), scales=w_scales[:, t, :], in_=w_grouped[:, t, :]
+            )
+
+        def multiply(t):
             first_col = (t * P) % BANK_COLS
-            if first_col == 0:
-                acc = psum_out.tile([P, BANK_COLS], F32)
-                acc_banks.append(acc)
             for g in range(PASSES):
                 cols = slice(g * P, (g + 1) * P)
                 nc.tensor.matmul_mx(
-                    out=acc_banks[-1][:, first_col : first_col + P],
+                    out=acc_banks[t * P // BANK_COLS][:, first_col : first_col + P],
                     lhsT=x_codes[:, cols].bitcast(FP8X4),
                     lhsT_scale=x_scales[:, cols],
-                    rhs=w_codes[:, cols].bitcast(FP8X4),
-                    rhs_scale=w_scales[:, cols],
+                    rhs=w_codes[:, t, cols].bitcast(FP8X4),
+                    rhs_scale=w_scales[:, t, cols],
                     start=(g == 0),
                     stop=(g == PASSES - 1),
                 )
 
+        for t in (3, 4, 5, 0, 1, 2, 6, 7):
+            quantise(t)
+            multiply(t)
+
         out_sb = keep.tile([P, D_OUT], F32)
-        for first_col in range(0, D_OUT, STORE_COLS):
-            o_cols = slice(first_col, first_col + STORE_COLS)
+        first_col = 0
+        for width in STORES:
+            o_cols = slice(first_col, first_col + width)
             in_bank = first_col % BANK_COLS
             nc.vector.tensor_tensor(
                 out=out_sb[:, o_cols],
-                in0=acc_banks[first_col // BANK_COLS][:, in_bank : in_bank + STORE_COLS],
+                in0=acc_banks[first_col // BANK_COLS][:, in_bank : in_bank + width],
                 in1=bias_sb[:, o_cols],
                 op=ALU.add,
             )
             nc.sync.dma_start(out=out_rows[:, o_cols], in_=out_sb[:, o_cols])
+            first_col = first_col + width

@@ -25,6 +25,7 @@ BANK_COLS = 512
 STORES = (256, 256, 256, 128, 128)
 MAGNITUDE_BITS = 0x7FFF7FFF
 STEEP = 2.0**100
+WARM_COLS = 384
 SUM_COLS = 16
 EARLY_TILES = (0, 1, 2)
 SCALAR_TILES = (0, 2, 4)
@@ -85,6 +86,8 @@ def tile_ternarylinear_s_kernel(tc, x, weight, alpha, bias, out):
         col_sums = psum_sum.tile([P, BANK_COLS], F32, tag="col_sums")
         ones = keep.tile([P, 1], BF16)
         nc.vector.memset(ones[:], 1.0)
+        warm_rows = keep.tile([P, WARM_COLS], F32)
+        nc.vector.memset(warm_rows[:], 0.0)
         table_loader = keep.tile([P, 1], BF16)
         nc.scalar.activation(out=table_loader[:], in_=ones[:], func=ACT.Sigmoid)
 
@@ -203,6 +206,13 @@ def tile_ternarylinear_s_kernel(tc, x, weight, alpha, bias, out):
         copy_grouped(nc, turned_x, x_grouped[:])
         copy_grouped(nc, turned_sign[2], early_sign[:, 2, :])
         add_to_delta(6, first=True, last=True)
+        nc.tensor.matmul(
+            out=col_sums[:, :WARM_COLS],
+            lhsT=mean_weights[:],
+            rhs=warm_rows[:],
+            start=True,
+            stop=True,
+        )
         twice_alpha = keep.tile([P, 1], F32)
         nc.vector.tensor_scalar(
             out=twice_alpha[:], in0=alpha_bf[:], scalar1=2.0, scalar2=None, op0=ALU.mult

@@ -73,8 +73,7 @@ def tile_ternarylinear_s_kernel(tc, x, weight, alpha, bias, out):
         ctx.enter_context(tc.manual_schedule())
         keep = ctx.enter_context(tc.tile_pool(name="keep", bufs=1))
         work = ctx.enter_context(tc.tile_pool(name="work", bufs=3))
-        psum_turn = ctx.enter_context(tc.psum_pool(name="psum_turn", bufs=4))
-        psum_out = ctx.enter_context(tc.psum_pool(name="psum_out", bufs=D_OUT // BANK_COLS))
+        psum_turn = ctx.enter_context(tc.psum_pool(name="psum_turn", bufs=6))
         psum_sum = ctx.enter_context(tc.psum_pool(name="psum_sum", bufs=1))
 
         ident = keep.tile([P, P], F32)
@@ -86,6 +85,10 @@ def tile_ternarylinear_s_kernel(tc, x, weight, alpha, bias, out):
         col_sums = psum_sum.tile([P, BANK_COLS], F32, tag="col_sums")
         ones = keep.tile([P, 1], BF16)
         nc.vector.memset(ones[:], 1.0)
+        alpha_column = keep.tile([P, 1], BF16)
+        nc.vector.memset(alpha_column[:], 0.0)
+        all_ones = keep.tile([P, P], BF16)
+        nc.vector.memset(all_ones[:], 1.0)
         warm_rows = keep.tile([P, WARM_COLS], F32)
         nc.vector.memset(warm_rows[:], 0.0)
         table_loader = keep.tile([P, 1], BF16)
@@ -103,10 +106,9 @@ def tile_ternarylinear_s_kernel(tc, x, weight, alpha, bias, out):
         w_sb = keep.tile([P, O_TILES, D_IN], BF16)
         for t in range(O_TILES):
             nc.sync.dma_start(out=w_sb[:, t, :], in_=w_tiles[t])
+        nc.scalar.dma_start(out=alpha_column[0:1, :], in_=alpha.partition_broadcast(1))
         x_sb = keep.tile([P, D_IN], BF16)
         nc.sync.dma_start(out=x_sb[:], in_=x_rows)
-        alpha_bf = keep.tile([P, 1], BF16)
-        nc.sync.dma_start(out=alpha_bf[:], in_=alpha.partition_broadcast(P))
         bias_sb = keep.tile([P, D_OUT], BF16)
         nc.sync.dma_start(out=bias_sb[:], in_=bias.partition_broadcast(P))
 
@@ -186,11 +188,15 @@ def tile_ternarylinear_s_kernel(tc, x, weight, alpha, bias, out):
         sign_of(2)
         abs_on_vector(3, whole)
         sum_on_tensor(3)
-        turn_sign(2)
+        turned_sign[2] = turn_in_order(nc, psum_turn, half_sign[:, 2, :], ident[:])
         sign_of(3)
         sign_of(4)
         abs_on_vector(5, whole)
         sum_on_tensor(5, last=True)
+        spread = psum_turn.tile([P, WORDS], F32, tag="turned")
+        nc.tensor.matmul(
+            out=spread[:, 0:1], lhsT=all_ones[:], rhs=alpha_column[:], start=True, stop=True
+        )
         sign_of(5)
         abs_on_vector(SHARED_TILE, vector_cols)
         sign_of(6)
@@ -198,13 +204,22 @@ def tile_ternarylinear_s_kernel(tc, x, weight, alpha, bias, out):
         nc.vector.tensor_copy(out=partial[:, 4:5], in_=col_sums[:, 0:1])
         abs_on_vector(LAST_TILE, whole)
         nc.vector.reduce_sum(out=partial[:, 7:8], in_=partial[:, 0:6], axis=mybir.AxisListType.X)
+        twice_alpha = keep.tile([P, 1], F32)
+        nc.vector.tensor_scalar(
+            out=twice_alpha[:], in0=spread[:, 0:1], scalar1=2.0, scalar2=None, op0=ALU.mult
+        )
         sign_of(7)
         sum_on_vector(LAST_TILE, whole, 6, initial=partial[:, 7:8])
         turned_x = turn(nc, psum_turn, x_sb[:], ident[:])
         copy_grouped(nc, turned_sign[0], early_sign[:, 0, :])
         copy_grouped(nc, turned_sign[1], early_sign[:, 1, :])
         copy_grouped(nc, turned_x, x_grouped[:])
-        copy_grouped(nc, turned_sign[2], early_sign[:, 2, :])
+        nc.scalar.activation(
+            out=early_alpha[:, 2, :],
+            in_=turned_sign[2][:].bitcast(BF16),
+            func=ACT.Copy,
+            scale=twice_alpha[:, 0:1],
+        )
         add_to_delta(6, first=True, last=True)
         nc.tensor.matmul(
             out=col_sums[:, :WARM_COLS],
@@ -212,10 +227,6 @@ def tile_ternarylinear_s_kernel(tc, x, weight, alpha, bias, out):
             rhs=warm_rows[:],
             start=True,
             stop=True,
-        )
-        twice_alpha = keep.tile([P, 1], F32)
-        nc.vector.tensor_scalar(
-            out=twice_alpha[:], in0=alpha_bf[:], scalar1=2.0, scalar2=None, op0=ALU.mult
         )
 
         def sign_to_alpha(t):
@@ -300,7 +311,6 @@ def tile_ternarylinear_s_kernel(tc, x, weight, alpha, bias, out):
         mask_on_vector(6)
         product_then_turn(5)
         turn_mask(2)
-        sign_to_alpha(2)
         product_of_turned(0)
         mask_on_vector(7)
         product_of_turned(1)
@@ -312,7 +322,7 @@ def tile_ternarylinear_s_kernel(tc, x, weight, alpha, bias, out):
         w_scales = keep.tile([P, O_TILES, CODE_COLS], U8, align_bytes=64)
         acc_banks = []
         for i in range(D_OUT // BANK_COLS):
-            acc = psum_out.tile([P, BANK_COLS], F32)
+            acc = psum_sum.tile([P, BANK_COLS], F32, tag=("col_sums", "delta")[i])
             acc_banks.append(acc)
 
         def quantise(t):

@@ -22,7 +22,7 @@ WORDS = D_IN // 2
 TURNS = WORDS // P
 CODE_COLS = PASSES * P
 BANK_COLS = 512
-STORES = (256, 256, 256, 128, 128)
+STORES = ((512, 256), (768, 256), (0, 256), (384, 128), (256, 128))
 MAGNITUDE_BITS = 0x7FFF7FFF
 STEEP = 2.0**100
 WARM_COLS = 384
@@ -298,25 +298,23 @@ def tile_ternarylinear_s_kernel(tc, x, weight, alpha, bias, out):
             )
             copy_grouped(nc, turn(nc, psum_turn, w_q[:], ident[:]), w_grouped[:, t, :])
 
-        mask_on_scalar(0)
-        mask_on_scalar(1)
+        for t in EARLY_TILES:
+            mask_on_scalar(t)
         mask_on_vector(3)
         mask_on_vector(4)
         product_then_turn(3)
         turn_mask(0)
-        mask_on_scalar(2)
         mask_on_vector(5)
         product_then_turn(4)
         turn_mask(1)
         mask_on_vector(6)
         product_then_turn(5)
         turn_mask(2)
-        product_of_turned(0)
         mask_on_vector(7)
-        product_of_turned(1)
         product_then_turn(6)
         product_then_turn(7)
-        product_of_turned(2)
+        for t in EARLY_TILES:
+            product_of_turned(t)
 
         w_codes = keep.tile([P, O_TILES, CODE_COLS], U32, align_bytes=64)
         w_scales = keep.tile([P, O_TILES, CODE_COLS], U8, align_bytes=64)
@@ -344,13 +342,12 @@ def tile_ternarylinear_s_kernel(tc, x, weight, alpha, bias, out):
                     stop=(g == PASSES - 1),
                 )
 
-        for t in (3, 4, 5, 0, 1, 2, 6, 7):
+        for t in (3, 4, 5, 6, 7, 0, 1, 2):
             quantise(t)
             multiply(t)
 
         out_sb = keep.tile([P, D_OUT], F32)
-        first_col = 0
-        for width in STORES:
+        for first_col, width in STORES:
             o_cols = slice(first_col, first_col + width)
             in_bank = first_col % BANK_COLS
             nc.vector.tensor_tensor(
@@ -360,4 +357,3 @@ def tile_ternarylinear_s_kernel(tc, x, weight, alpha, bias, out):
                 op=ALU.add,
             )
             nc.sync.dma_start(out=out_rows[:, o_cols], in_=out_sb[:, o_cols])
-            first_col = first_col + width

@@ -31,7 +31,7 @@ EARLY_TILES = (0, 1, 2)
 SCALAR_TILES = (0, 2, 4)
 TENSOR_TILES = (1, 3, 5)
 SHARED_TILE = 6
-VECTOR_COLS = 384
+VECTOR_COLS = 512
 LAST_TILE = 7
 
 FLOPS = 2 * P * D_IN * D_OUT
@@ -202,12 +202,12 @@ def tile_ternarylinear_s_kernel(tc, x, weight, alpha, bias, out):
         sign_of(6)
         sum_on_vector(SHARED_TILE, vector_cols, 5)
         nc.vector.tensor_copy(out=partial[:, 4:5], in_=col_sums[:, 0:1])
-        abs_on_vector(LAST_TILE, whole)
-        nc.vector.reduce_sum(out=partial[:, 7:8], in_=partial[:, 0:6], axis=mybir.AxisListType.X)
         twice_alpha = keep.tile([P, 1], F32)
         nc.vector.tensor_scalar(
             out=twice_alpha[:], in0=spread[:, 0:1], scalar1=2.0, scalar2=None, op0=ALU.mult
         )
+        abs_on_vector(LAST_TILE, whole)
+        nc.vector.reduce_sum(out=partial[:, 7:8], in_=partial[:, 0:6], axis=mybir.AxisListType.X)
         sign_of(7)
         sum_on_vector(LAST_TILE, whole, 6, initial=partial[:, 7:8])
         turned_x = turn(nc, psum_turn, x_sb[:], ident[:])
@@ -221,13 +221,17 @@ def tile_ternarylinear_s_kernel(tc, x, weight, alpha, bias, out):
             scale=twice_alpha[:, 0:1],
         )
         add_to_delta(6, first=True, last=True)
-        nc.tensor.matmul(
-            out=col_sums[:, :WARM_COLS],
-            lhsT=mean_weights[:],
-            rhs=warm_rows[:],
-            start=True,
-            stop=True,
-        )
+
+        def keep_clock_up():
+            nc.tensor.matmul(
+                out=col_sums[:, :WARM_COLS],
+                lhsT=mean_weights[:],
+                rhs=warm_rows[:],
+                start=True,
+                stop=True,
+            )
+
+        keep_clock_up()
 
         def sign_to_alpha(t):
             nc.vector.tensor_scalar(
@@ -257,17 +261,17 @@ def tile_ternarylinear_s_kernel(tc, x, weight, alpha, bias, out):
         mask_of = {}
         turned_mask_of = {}
 
-        def mask_on_vector(t):
-            mask = work.tile([P, D_IN], BF16, tag="mask")
+        own_mask = keep.tile([P, O_TILES, D_IN], BF16)
+
+        def mask_on_vector(tiles):
             nc.vector.tensor_scalar(
-                out=mask[:],
-                in0=magnitude[:, t, :],
+                out=own_mask[:, tiles, :],
+                in0=magnitude[:, tiles, :],
                 scalar1=delta[:, 0:1],
                 scalar2=twice_alpha[:, 0:1],
                 op0=ALU.is_gt,
                 op1=ALU.mult,
             )
-            mask_of[t] = mask
 
         def mask_on_scalar(t):
             mask = work.tile([P, D_IN], BF16, tag="scalar_mask")
@@ -294,25 +298,24 @@ def tile_ternarylinear_s_kernel(tc, x, weight, alpha, bias, out):
         def product_then_turn(t):
             w_q = work.tile([P, D_IN], BF16, tag="w_q")
             nc.vector.tensor_tensor(
-                out=w_q[:], in0=mask_of[t][:], in1=half_sign[:, t, :], op=ALU.mult
+                out=w_q[:], in0=own_mask[:, t, :], in1=half_sign[:, t, :], op=ALU.mult
             )
             copy_grouped(nc, turn(nc, psum_turn, w_q[:], ident[:]), w_grouped[:, t, :])
 
         for t in EARLY_TILES:
             mask_on_scalar(t)
-        mask_on_vector(3)
-        mask_on_vector(4)
+        mask_on_vector(slice(3, 4))
+        mask_on_vector(slice(4, 6))
         product_then_turn(3)
         turn_mask(0)
-        mask_on_vector(5)
         product_then_turn(4)
         turn_mask(1)
-        mask_on_vector(6)
+        mask_on_vector(slice(6, 8))
         product_then_turn(5)
         turn_mask(2)
-        mask_on_vector(7)
         product_then_turn(6)
         product_then_turn(7)
+        keep_clock_up()
         for t in EARLY_TILES:
             product_of_turned(t)
 

@@ -22,17 +22,10 @@ WORDS = D_IN // 2
 TURNS = WORDS // P
 CODE_COLS = PASSES * P
 BANK_COLS = 512
-STORES = ((512, 256), (768, 256), (0, 256), (384, 128), (256, 128))
 MAGNITUDE_BITS = 0x7FFF7FFF
-STEEP = 2.0**100
-WARM_COLS = 384
+TERNARY_BITS = -0x3FFF4000
+EDGE = (2.0 - 2.0**-8) * (1.0 - 2.0**-22)
 SUM_COLS = 16
-EARLY_TILES = (0, 1, 2)
-SCALAR_TILES = (0, 2, 4)
-TENSOR_TILES = (1, 3, 5)
-SHARED_TILE = 6
-VECTOR_COLS = 512
-LAST_TILE = 7
 
 FLOPS = 2 * P * D_IN * D_OUT
 
@@ -73,35 +66,24 @@ def tile_ternarylinear_s_kernel(tc, x, weight, alpha, bias, out):
         ctx.enter_context(tc.manual_schedule())
         keep = ctx.enter_context(tc.tile_pool(name="keep", bufs=1))
         work = ctx.enter_context(tc.tile_pool(name="work", bufs=3))
-        psum_turn = ctx.enter_context(tc.psum_pool(name="psum_turn", bufs=6))
+        psum_turn = ctx.enter_context(tc.psum_pool(name="psum_turn", bufs=7))
         psum_sum = ctx.enter_context(tc.psum_pool(name="psum_sum", bufs=1))
 
         ident = keep.tile([P, P], F32)
         make_identity(nc, ident[:])
         mean_weights = keep.tile([P, P], F32)
-        nc.vector.memset(mean_weights[:], 0.7 / (D_OUT * D_IN))
+        nc.vector.memset(mean_weights[:], 0.7 / (D_OUT * D_IN) / EDGE)
         partial = keep.tile([P, SUM_COLS], F32)
+        nc.vector.memset(partial[:], 2.0**-100)
         delta = psum_sum.tile([P, BANK_COLS], F32, tag="delta")
-        col_sums = psum_sum.tile([P, BANK_COLS], F32, tag="col_sums")
         ones = keep.tile([P, 1], BF16)
         nc.vector.memset(ones[:], 1.0)
         alpha_column = keep.tile([P, 1], BF16)
         nc.vector.memset(alpha_column[:], 0.0)
         all_ones = keep.tile([P, P], BF16)
         nc.vector.memset(all_ones[:], 1.0)
-        warm_rows = keep.tile([P, WARM_COLS], F32)
-        nc.vector.memset(warm_rows[:], 0.0)
         table_loader = keep.tile([P, 1], BF16)
-        nc.scalar.activation(out=table_loader[:], in_=ones[:], func=ACT.Sigmoid)
-
-        def add_to_delta(col, first=False, last=False):
-            nc.tensor.matmul(
-                out=delta[:, 0:1],
-                lhsT=mean_weights[:],
-                rhs=partial[:, col : col + 1],
-                start=first,
-                stop=last,
-            )
+        nc.scalar.activation(out=table_loader[:], in_=ones[:], func=ACT.Abs)
 
         w_sb = keep.tile([P, O_TILES, D_IN], BF16)
         for t in range(O_TILES):
@@ -113,17 +95,7 @@ def tile_ternarylinear_s_kernel(tc, x, weight, alpha, bias, out):
         nc.sync.dma_start(out=bias_sb[:], in_=bias.partition_broadcast(P))
 
         magnitude = keep.tile([P, O_TILES, D_IN], BF16)
-        half_sign = keep.tile([P, O_TILES, D_IN], BF16)
-
-        def sign_of(t):
-            nc.vector.tensor_scalar(
-                out=half_sign[:, t, :],
-                in0=w_sb[:, t, :],
-                scalar1=0.0,
-                scalar2=0.5,
-                op0=ALU.is_ge,
-                op1=ALU.subtract,
-            )
+        w_grouped = keep.tile([P, O_TILES, D_IN], BF16, align_bytes=64)
 
         def abs_on_vector(t, cols):
             nc.vector.tensor_scalar(
@@ -134,7 +106,7 @@ def tile_ternarylinear_s_kernel(tc, x, weight, alpha, bias, out):
                 op0=ALU.bitwise_and,
             )
 
-        def abs_and_sum_on_scalar(t, cols, sum_col):
+        def sum_on_scalar(t, cols, sum_col):
             nc.scalar.activation(
                 out=magnitude[:, t, cols],
                 in_=w_sb[:, t, cols],
@@ -154,189 +126,117 @@ def tile_ternarylinear_s_kernel(tc, x, weight, alpha, bias, out):
                 accum_out=partial[:, sum_col : sum_col + 1],
             )
 
+        turned = {}
+
+        def copy_turned(t):
+            copy_grouped(nc, turned[t], w_grouped[:, t, :])
+
         whole = slice(0, D_IN)
-        vector_cols = slice(0, VECTOR_COLS)
-        scalar_cols = slice(VECTOR_COLS, D_IN)
-        def sum_on_tensor(t, first=False, last=False):
-            for j in range(D_IN // P):
-                nc.tensor.matmul(
-                    out=col_sums[:, 0:1],
-                    lhsT=magnitude[:, t, j * P : (j + 1) * P],
-                    rhs=ones[:],
-                    start=(first and j == 0),
-                    stop=(last and j == D_IN // P - 1),
-                )
-
-        early_sign = keep.tile([P, len(EARLY_TILES), D_IN], BF16, align_bytes=64)
-        early_alpha = keep.tile([P, len(EARLY_TILES), D_IN], BF16, align_bytes=64)
-        x_grouped = keep.tile([P, D_IN], BF16, align_bytes=64)
-        turned_sign = {}
-
-        def turn_sign(t):
-            turned_sign[t] = turn(nc, psum_turn, half_sign[:, t, :], ident[:])
-
-        for i in range(3):
-            abs_and_sum_on_scalar(SCALAR_TILES[i], whole, i)
-        abs_and_sum_on_scalar(SHARED_TILE, scalar_cols, 3)
-
-        sign_of(0)
-        turn_sign(0)
-        abs_on_vector(1, whole)
-        sum_on_tensor(1, first=True)
-        sign_of(1)
-        turn_sign(1)
-        sign_of(2)
-        abs_on_vector(3, whole)
-        sum_on_tensor(3)
-        turned_sign[2] = turn_in_order(nc, psum_turn, half_sign[:, 2, :], ident[:])
-        sign_of(3)
-        sign_of(4)
-        abs_on_vector(5, whole)
-        sum_on_tensor(5, last=True)
-        spread = psum_turn.tile([P, WORDS], F32, tag="turned")
-        nc.tensor.matmul(
-            out=spread[:, 0:1], lhsT=all_ones[:], rhs=alpha_column[:], start=True, stop=True
-        )
-        sign_of(5)
-        abs_on_vector(SHARED_TILE, vector_cols)
-        sign_of(6)
-        sum_on_vector(SHARED_TILE, vector_cols, 5)
-        nc.vector.tensor_copy(out=partial[:, 4:5], in_=col_sums[:, 0:1])
-        twice_alpha = keep.tile([P, 1], F32)
-        nc.vector.tensor_scalar(
-            out=twice_alpha[:], in0=spread[:, 0:1], scalar1=2.0, scalar2=None, op0=ALU.mult
-        )
-        abs_on_vector(LAST_TILE, whole)
-        nc.vector.reduce_sum(out=partial[:, 7:8], in_=partial[:, 0:6], axis=mybir.AxisListType.X)
-        sign_of(7)
-        sum_on_vector(LAST_TILE, whole, 6, initial=partial[:, 7:8])
-        turned_x = turn(nc, psum_turn, x_sb[:], ident[:])
-        copy_grouped(nc, turned_sign[0], early_sign[:, 0, :])
-        copy_grouped(nc, turned_sign[1], early_sign[:, 1, :])
-        copy_grouped(nc, turned_x, x_grouped[:])
-        nc.scalar.activation(
-            out=early_alpha[:, 2, :],
-            in_=turned_sign[2][:].bitcast(BF16),
-            func=ACT.Copy,
-            scale=twice_alpha[:, 0:1],
-        )
-        add_to_delta(6, first=True, last=True)
-
-        def keep_clock_up():
+        first_half = slice(0, D_IN // 2)
+        second_half = slice(D_IN // 2, D_IN)
+        def add_to_delta(col, first=False, last=False):
             nc.tensor.matmul(
-                out=col_sums[:, :WARM_COLS],
+                out=delta[:, 0:1],
                 lhsT=mean_weights[:],
-                rhs=warm_rows[:],
-                start=True,
-                stop=True,
+                rhs=partial[:, col : col + 1],
+                start=first,
+                stop=last,
             )
 
-        keep_clock_up()
+        for t, col in ((0, 0), (2, 1), (4, 5), (6, 6)):
+            sum_on_scalar(t, whole, col)
+        for t in (0, 1):
+            turned[t] = turn(nc, psum_turn, w_sb[:, t, :], ident[:])
+            copy_turned(t)
+        for t in (2, 3, 4):
+            turned[t] = turn_in_order(nc, psum_turn, w_sb[:, t, :], ident[:])
+        nc.tensor.matmul(
+            out=delta[:, 1:2], lhsT=all_ones[:], rhs=alpha_column[:], start=True, stop=True
+        )
+        turned[5] = turn_in_order(nc, psum_turn, w_sb[:, 5, :], ident[:])
+        half_alpha = keep.tile([P, 1], F32)
+        abs_on_vector(1, whole)
+        sum_on_vector(1, whole, 4)
+        abs_on_vector(3, whole)
+        sum_on_vector(3, whole, 2, initial=partial[:, 4:5])
+        abs_on_vector(5, whole)
+        nc.vector.reduce_sum(out=partial[:, 8:9], in_=partial[:, 0:4], axis=mybir.AxisListType.X)
+        nc.vector.tensor_scalar(
+            out=half_alpha[:], in0=delta[:, 1:2], scalar1=0.5, scalar2=None, op0=ALU.mult
+        )
+        sum_on_vector(5, whole, 7, initial=partial[:, 8:9])
+        abs_on_vector(7, whole)
+        sum_on_vector(7, whole, 9, initial=partial[:, 7:8])
+        add_to_delta(5, first=True)
+        turned_x = turn(nc, psum_turn, x_sb[:], ident[:])
+        add_to_delta(6)
+        add_to_delta(9, last=True)
+        for t in (6, 7):
+            turned[t] = turn_in_order(nc, psum_turn, w_sb[:, t, :], ident[:])
+        x_grouped = keep.tile([P, D_IN], BF16, align_bytes=64)
+        nc.vector.tensor_copy(
+            out=x_grouped[:].bitcast(F32).rearrange("p (g r u) -> p g r u", g=PASSES, u=2),
+            in_=turned_x[:].rearrange("p (g u) r -> p g r u", u=2),
+        )
+        to_edge = keep.tile([P, 1], F32)
+        nc.vector.reciprocal(out=to_edge[:], in_=delta[:, 0:1])
 
-        def sign_to_alpha(t):
+        scaled = keep.tile([P, O_TILES, D_IN], BF16, align_bytes=64)
+        ternary = keep.tile([P, O_TILES, D_IN], BF16, align_bytes=64)
+        w_q = keep.tile([P, O_TILES, D_IN], BF16, align_bytes=64)
+
+        def scale_on_vector(t):
             nc.vector.tensor_scalar(
-                out=early_alpha[:, t, :],
-                in0=early_sign[:, t, :],
-                scalar1=twice_alpha[:, 0:1],
+                out=scaled[:, t, :],
+                in0=w_grouped[:, t, :],
+                scalar1=to_edge[:, 0:1],
                 scalar2=None,
                 op0=ALU.mult,
             )
 
-        sign_to_alpha(0)
-        sign_to_alpha(1)
+        def scale_on_scalar(t):
+            nc.scalar.activation(
+                out=scaled[:, t, :],
+                in_=turned[t][:].bitcast(BF16),
+                func=ACT.Copy,
+                scale=to_edge[:, 0:1],
+            )
+
+        def to_ternary(t):
+            nc.vector.tensor_scalar(
+                out=ternary[:, t, :].bitcast(I32),
+                in0=scaled[:, t, :].bitcast(I32),
+                scalar1=TERNARY_BITS,
+                scalar2=None,
+                op0=ALU.bitwise_and,
+            )
+
+        def times_alpha(t):
+            nc.vector.tensor_scalar(
+                out=w_q[:, t, :],
+                in0=ternary[:, t, :],
+                scalar1=half_alpha[:, 0:1],
+                scalar2=None,
+                op0=ALU.mult,
+            )
+
         x_codes = keep.tile([P, CODE_COLS], U32, align_bytes=64)
         x_scales = keep.tile([P, CODE_COLS], U8, align_bytes=64)
-        nc.vector.quantize_mx(out=x_codes[:].bitcast(FP8X4), scales=x_scales[:], in_=x_grouped[:])
-        step_bias = keep.tile([P, 1], F32)
-        nc.vector.tensor_scalar(
-            out=step_bias[:],
-            in0=delta[:, 0:1],
-            scalar1=-STEEP * (1.0 + 2.0**-22),
-            scalar2=-1000.0,
-            op0=ALU.mult,
-            op1=ALU.add,
-        )
-
-        w_grouped = keep.tile([P, O_TILES, D_IN], BF16, align_bytes=64)
-        mask_of = {}
-        turned_mask_of = {}
-
-        own_mask = keep.tile([P, O_TILES, D_IN], BF16)
-
-        def mask_on_vector(tiles):
-            nc.vector.tensor_scalar(
-                out=own_mask[:, tiles, :],
-                in0=magnitude[:, tiles, :],
-                scalar1=delta[:, 0:1],
-                scalar2=twice_alpha[:, 0:1],
-                op0=ALU.is_gt,
-                op1=ALU.mult,
-            )
-
-        def mask_on_scalar(t):
-            mask = work.tile([P, D_IN], BF16, tag="scalar_mask")
-            nc.scalar.activation(
-                out=mask[:],
-                in_=magnitude[:, t, :],
-                func=ACT.Sigmoid,
-                scale=STEEP,
-                bias=step_bias[:, 0:1],
-            )
-            mask_of[t] = mask
-
-        def turn_mask(t):
-            turned_mask_of[t] = turn_in_order(nc, psum_turn, mask_of[t][:], ident[:])
-
-        def product_of_turned(t):
-            nc.vector.tensor_tensor(
-                out=w_grouped[:, t, :],
-                in0=turned_mask_of[t][:].bitcast(BF16),
-                in1=early_alpha[:, t, :],
-                op=ALU.mult,
-            )
-
-        def product_then_turn(t):
-            w_q = work.tile([P, D_IN], BF16, tag="w_q")
-            nc.vector.tensor_tensor(
-                out=w_q[:], in0=own_mask[:, t, :], in1=half_sign[:, t, :], op=ALU.mult
-            )
-            copy_grouped(nc, turn(nc, psum_turn, w_q[:], ident[:]), w_grouped[:, t, :])
-
-        for t in EARLY_TILES:
-            mask_on_scalar(t)
-        mask_on_vector(slice(3, 4))
-        mask_on_vector(slice(4, 6))
-        product_then_turn(3)
-        turn_mask(0)
-        product_then_turn(4)
-        turn_mask(1)
-        mask_on_vector(slice(6, 8))
-        product_then_turn(5)
-        turn_mask(2)
-        product_then_turn(6)
-        product_then_turn(7)
-        keep_clock_up()
-        for t in EARLY_TILES:
-            product_of_turned(t)
-
         w_codes = keep.tile([P, O_TILES, CODE_COLS], U32, align_bytes=64)
         w_scales = keep.tile([P, O_TILES, CODE_COLS], U8, align_bytes=64)
-        acc_banks = []
-        for i in range(D_OUT // BANK_COLS):
-            acc = psum_sum.tile([P, BANK_COLS], F32, tag=("col_sums", "delta")[i])
-            acc_banks.append(acc)
+        out_sb = keep.tile([P, D_OUT], F32)
 
         def quantise(t):
             nc.vector.quantize_mx(
-                out=w_codes[:, t, :].bitcast(FP8X4), scales=w_scales[:, t, :], in_=w_grouped[:, t, :]
+                out=w_codes[:, t, :].bitcast(FP8X4), scales=w_scales[:, t, :], in_=w_q[:, t, :]
             )
 
-        def multiply(t):
-            first_col = (t * P) % BANK_COLS
+        def multiply(t, acc):
+            first_col = (t % 2) * P
             for g in range(PASSES):
                 cols = slice(g * P, (g + 1) * P)
                 nc.tensor.matmul_mx(
-                    out=acc_banks[t * P // BANK_COLS][:, first_col : first_col + P],
+                    out=acc[:, first_col : first_col + P],
                     lhsT=x_codes[:, cols].bitcast(FP8X4),
                     lhsT_scale=x_scales[:, cols],
                     rhs=w_codes[:, t, cols].bitcast(FP8X4),
@@ -345,18 +245,62 @@ def tile_ternarylinear_s_kernel(tc, x, weight, alpha, bias, out):
                     stop=(g == PASSES - 1),
                 )
 
-        for t in (3, 4, 5, 6, 7, 0, 1, 2):
-            quantise(t)
-            multiply(t)
-
-        out_sb = keep.tile([P, D_OUT], F32)
-        for first_col, width in STORES:
+        def add_bias_and_store(acc, first_col, width):
             o_cols = slice(first_col, first_col + width)
-            in_bank = first_col % BANK_COLS
+            in_bank = first_col % (2 * P)
             nc.vector.tensor_tensor(
                 out=out_sb[:, o_cols],
-                in0=acc_banks[first_col // BANK_COLS][:, in_bank : in_bank + width],
+                in0=acc[:, in_bank : in_bank + width],
                 in1=bias_sb[:, o_cols],
                 op=ALU.add,
             )
             nc.sync.dma_start(out=out_rows[:, o_cols], in_=out_sb[:, o_cols])
+
+        for t in range(2, O_TILES):
+            scale_on_scalar(t)
+
+        scale_on_vector(0)
+        scale_on_vector(1)
+        to_ternary(0)
+        to_ternary(1)
+        times_alpha(0)
+        times_alpha(1)
+        nc.vector.quantize_mx(out=x_codes[:].bitcast(FP8X4), scales=x_scales[:], in_=x_grouped[:])
+        quantise(0)
+        quantise(1)
+        acc_01 = psum_turn.tile([P, WORDS], F32, tag="turned")
+        multiply(0, acc_01)
+        multiply(1, acc_01)
+        to_ternary(2)
+        to_ternary(3)
+        times_alpha(2)
+        times_alpha(3)
+        quantise(2)
+        quantise(3)
+        acc_23 = psum_turn.tile([P, WORDS], F32, tag="turned")
+        multiply(2, acc_23)
+        multiply(3, acc_23)
+        to_ternary(4)
+        add_bias_and_store(acc_01, 0, 2 * P)
+        times_alpha(4)
+        to_ternary(5)
+        quantise(4)
+        times_alpha(5)
+        add_bias_and_store(acc_23, 2 * P, 2 * P)
+        quantise(5)
+        acc_45 = psum_turn.tile([P, WORDS], F32, tag="turned")
+        multiply(4, acc_45)
+        multiply(5, acc_45)
+        to_ternary(6)
+        to_ternary(7)
+        times_alpha(6)
+        times_alpha(7)
+        quantise(6)
+        quantise(7)
+        acc_6 = psum_turn.tile([P, WORDS], F32, tag="turned")
+        multiply(6, acc_6)
+        add_bias_and_store(acc_45, 4 * P, 2 * P)
+        acc_7 = psum_turn.tile([P, WORDS], F32, tag="turned")
+        multiply(7, acc_7)
+        add_bias_and_store(acc_6, 6 * P, P)
+        add_bias_and_store(acc_7, 7 * P, P)

@@ -145,10 +145,10 @@ def tile_ternarylinear_s_kernel(tc, x, weight, alpha, bias, out):
 
         for t, col in ((0, 0), (2, 1), (4, 5), (6, 6)):
             sum_on_scalar(t, whole, col)
-        for t in (0, 1):
+        for t in (0, 1, 2):
             turned[t] = turn(nc, psum_turn, w_sb[:, t, :], ident[:])
             copy_turned(t)
-        for t in (2, 3, 4):
+        for t in (3, 4):
             turned[t] = turn_in_order(nc, psum_turn, w_sb[:, t, :], ident[:])
         nc.tensor.matmul(
             out=delta[:, 1:2], lhsT=all_ones[:], rhs=alpha_column[:], start=True, stop=True
@@ -202,22 +202,30 @@ def tile_ternarylinear_s_kernel(tc, x, weight, alpha, bias, out):
                 scale=to_edge[:, 0:1],
             )
 
-        def to_ternary(t):
+        def tiles(first, count=1):
+            return slice(first, first + count)
+
+        def to_ternary(ts):
             nc.vector.tensor_scalar(
-                out=ternary[:, t, :].bitcast(I32),
-                in0=scaled[:, t, :].bitcast(I32),
+                out=ternary[:, ts, :].bitcast(I32),
+                in0=scaled[:, ts, :].bitcast(I32),
                 scalar1=TERNARY_BITS,
                 scalar2=None,
                 op0=ALU.bitwise_and,
             )
 
-        def times_alpha(t):
+        def times_alpha(ts):
             nc.vector.tensor_scalar(
-                out=w_q[:, t, :],
-                in0=ternary[:, t, :],
+                out=w_q[:, ts, :],
+                in0=ternary[:, ts, :],
                 scalar1=half_alpha[:, 0:1],
                 scalar2=None,
                 op0=ALU.mult,
+            )
+
+        def times_alpha_on_scalar(t):
+            nc.scalar.activation(
+                out=w_q[:, t, :], in_=ternary[:, t, :], func=ACT.Copy, scale=half_alpha[:, 0:1]
             )
 
         x_codes = keep.tile([P, CODE_COLS], U32, align_bytes=64)
@@ -226,17 +234,21 @@ def tile_ternarylinear_s_kernel(tc, x, weight, alpha, bias, out):
         w_scales = keep.tile([P, O_TILES, CODE_COLS], U8, align_bytes=64)
         out_sb = keep.tile([P, D_OUT], F32)
 
-        def quantise(t):
+        def quantise(ts):
             nc.vector.quantize_mx(
-                out=w_codes[:, t, :].bitcast(FP8X4), scales=w_scales[:, t, :], in_=w_q[:, t, :]
+                out=w_codes[:, ts, :].rearrange("p t c -> p (t c)").bitcast(FP8X4),
+                scales=w_scales[:, ts, :].rearrange("p t c -> p (t c)"),
+                in_=w_q[:, ts, :].rearrange("p t d -> p (t d)"),
             )
 
-        def multiply(t, acc):
-            first_col = (t % 2) * P
+        def new_bank():
+            return psum_turn.tile([P, WORDS], F32, tag="turned", name="products")
+
+        def multiply(t, bank, place):
             for g in range(PASSES):
                 cols = slice(g * P, (g + 1) * P)
                 nc.tensor.matmul_mx(
-                    out=acc[:, first_col : first_col + P],
+                    out=bank[:, place * P : (place + 1) * P],
                     lhsT=x_codes[:, cols].bitcast(FP8X4),
                     lhsT_scale=x_scales[:, cols],
                     rhs=w_codes[:, t, cols].bitcast(FP8X4),
@@ -245,62 +257,58 @@ def tile_ternarylinear_s_kernel(tc, x, weight, alpha, bias, out):
                     stop=(g == PASSES - 1),
                 )
 
-        def add_bias_and_store(acc, first_col, width):
-            o_cols = slice(first_col, first_col + width)
-            in_bank = first_col % (2 * P)
+        def add_bias_and_store(bank, first_tile, count):
+            o_cols = slice(first_tile * P, (first_tile + count) * P)
             nc.vector.tensor_tensor(
                 out=out_sb[:, o_cols],
-                in0=acc[:, in_bank : in_bank + width],
+                in0=bank[:, : count * P],
                 in1=bias_sb[:, o_cols],
                 op=ALU.add,
             )
             nc.sync.dma_start(out=out_rows[:, o_cols], in_=out_sb[:, o_cols])
 
-        for t in range(2, O_TILES):
+        for t in range(3, O_TILES):
             scale_on_scalar(t)
 
-        scale_on_vector(0)
-        scale_on_vector(1)
-        to_ternary(0)
-        to_ternary(1)
-        times_alpha(0)
-        times_alpha(1)
         nc.vector.quantize_mx(out=x_codes[:].bitcast(FP8X4), scales=x_scales[:], in_=x_grouped[:])
-        quantise(0)
-        quantise(1)
-        acc_01 = psum_turn.tile([P, WORDS], F32, tag="turned")
-        multiply(0, acc_01)
-        multiply(1, acc_01)
-        to_ternary(2)
-        to_ternary(3)
-        times_alpha(2)
-        times_alpha(3)
-        quantise(2)
-        quantise(3)
-        acc_23 = psum_turn.tile([P, WORDS], F32, tag="turned")
-        multiply(2, acc_23)
-        multiply(3, acc_23)
-        to_ternary(4)
-        add_bias_and_store(acc_01, 0, 2 * P)
-        times_alpha(4)
-        to_ternary(5)
-        quantise(4)
-        times_alpha(5)
-        add_bias_and_store(acc_23, 2 * P, 2 * P)
-        quantise(5)
-        acc_45 = psum_turn.tile([P, WORDS], F32, tag="turned")
-        multiply(4, acc_45)
-        multiply(5, acc_45)
-        to_ternary(6)
-        to_ternary(7)
-        times_alpha(6)
-        times_alpha(7)
-        quantise(6)
-        quantise(7)
-        acc_6 = psum_turn.tile([P, WORDS], F32, tag="turned")
-        multiply(6, acc_6)
-        add_bias_and_store(acc_45, 4 * P, 2 * P)
-        acc_7 = psum_turn.tile([P, WORDS], F32, tag="turned")
-        multiply(7, acc_7)
-        add_bias_and_store(acc_6, 6 * P, P)
-        add_bias_and_store(acc_7, 7 * P, P)
+        for t in (0, 1, 2):
+            scale_on_vector(t)
+        to_ternary(tiles(0, 2))
+        to_ternary(tiles(2))
+        times_alpha_on_scalar(2)
+        times_alpha(tiles(0, 2))
+        to_ternary(tiles(3))
+        quantise(tiles(0, 2))
+        bank_01 = new_bank()
+        multiply(0, bank_01, 0)
+        multiply(1, bank_01, 1)
+        times_alpha(tiles(3))
+        to_ternary(tiles(4))
+        quantise(tiles(3))
+        bank_34 = new_bank()
+        multiply(3, bank_34, 0)
+        times_alpha(tiles(4))
+        to_ternary(tiles(5))
+        add_bias_and_store(bank_01, 0, 2)
+        quantise(tiles(4))
+        multiply(4, bank_34, 1)
+        times_alpha(tiles(5))
+        to_ternary(tiles(6))
+        quantise(tiles(5))
+        bank_56 = new_bank()
+        multiply(5, bank_56, 0)
+        times_alpha(tiles(6))
+        to_ternary(tiles(7))
+        quantise(tiles(6))
+        multiply(6, bank_56, 1)
+        times_alpha(tiles(7))
+        quantise(tiles(2))
+        bank_2 = new_bank()
+        multiply(2, bank_2, 0)
+        quantise(tiles(7))
+        bank_7 = new_bank()
+        multiply(7, bank_7, 0)
+        add_bias_and_store(bank_34, 3, 2)
+        add_bias_and_store(bank_56, 5, 2)
+        add_bias_and_store(bank_2, 2, 1)
+        add_bias_and_store(bank_7, 7, 1)

@@ -148,12 +148,10 @@ def tile_ternarylinear_s_kernel(tc, x, weight, alpha, bias, out):
         for t in (0, 1, 2):
             turned[t] = turn(nc, psum_turn, w_sb[:, t, :], ident[:])
             copy_turned(t)
-        for t in (3, 4):
-            turned[t] = turn_in_order(nc, psum_turn, w_sb[:, t, :], ident[:])
+        turned[3] = turn_in_order(nc, psum_turn, w_sb[:, 3, :], ident[:])
         nc.tensor.matmul(
             out=delta[:, 1:2], lhsT=all_ones[:], rhs=alpha_column[:], start=True, stop=True
         )
-        turned[5] = turn_in_order(nc, psum_turn, w_sb[:, 5, :], ident[:])
         half_alpha = keep.tile([P, 1], F32)
         abs_on_vector(1, whole)
         sum_on_vector(1, whole, 4)
@@ -171,7 +169,7 @@ def tile_ternarylinear_s_kernel(tc, x, weight, alpha, bias, out):
         turned_x = turn(nc, psum_turn, x_sb[:], ident[:])
         add_to_delta(6)
         add_to_delta(9, last=True)
-        for t in (6, 7):
+        for t in (4, 5, 6, 7):
             turned[t] = turn_in_order(nc, psum_turn, w_sb[:, t, :], ident[:])
         x_grouped = keep.tile([P, D_IN], BF16, align_bytes=64)
         nc.vector.tensor_copy(

@@ -166,16 +166,12 @@ def tile_ternarylinear_s_kernel(tc, x, weight, alpha, bias, out):
         abs_on_vector(7, whole)
         sum_on_vector(7, whole, 9, initial=partial[:, 7:8])
         add_to_delta(5, first=True)
-        turned_x = turn(nc, psum_turn, x_sb[:], ident[:])
         add_to_delta(6)
         add_to_delta(9, last=True)
+        turned_x = turn(nc, psum_turn, x_sb[:], ident[:])
         for t in (4, 5, 6, 7):
             turned[t] = turn_in_order(nc, psum_turn, w_sb[:, t, :], ident[:])
         x_grouped = keep.tile([P, D_IN], BF16, align_bytes=64)
-        nc.vector.tensor_copy(
-            out=x_grouped[:].bitcast(F32).rearrange("p (g r u) -> p g r u", g=PASSES, u=2),
-            in_=turned_x[:].rearrange("p (g u) r -> p g r u", u=2),
-        )
         to_edge = keep.tile([P, 1], F32)
         nc.vector.reciprocal(out=to_edge[:], in_=delta[:, 0:1])
 
@@ -265,10 +261,11 @@ def tile_ternarylinear_s_kernel(tc, x, weight, alpha, bias, out):
             )
             nc.sync.dma_start(out=out_rows[:, o_cols], in_=out_sb[:, o_cols])
 
-        for t in range(3, O_TILES):
+        scale_on_scalar(3)
+        copy_grouped(nc, turned_x, x_grouped[:])
+        for t in range(4, O_TILES):
             scale_on_scalar(t)
 
-        nc.vector.quantize_mx(out=x_codes[:].bitcast(FP8X4), scales=x_scales[:], in_=x_grouped[:])
         for t in (0, 1, 2):
             scale_on_vector(t)
         to_ternary(tiles(0, 2))
@@ -276,11 +273,12 @@ def tile_ternarylinear_s_kernel(tc, x, weight, alpha, bias, out):
         times_alpha_on_scalar(2)
         times_alpha(tiles(0, 2))
         to_ternary(tiles(3))
+        nc.vector.quantize_mx(out=x_codes[:].bitcast(FP8X4), scales=x_scales[:], in_=x_grouped[:])
+        times_alpha(tiles(3))
         quantise(tiles(0, 2))
         bank_01 = new_bank()
         multiply(0, bank_01, 0)
         multiply(1, bank_01, 1)
-        times_alpha(tiles(3))
         to_ternary(tiles(4))
         quantise(tiles(3))
         bank_34 = new_bank()

@@ -25,6 +25,7 @@ BANK_COLS = 512
 MAGNITUDE_BITS = 0x7FFF7FFF
 TERNARY_BITS = -0x3FFF4000
 EDGE = (2.0 - 2.0**-8) * (1.0 - 2.0**-22)
+WARM_COLS = 512
 SUM_COLS = 16
 
 FLOPS = 2 * P * D_IN * D_OUT
@@ -82,6 +83,8 @@ def tile_ternarylinear_s_kernel(tc, x, weight, alpha, bias, out):
         nc.vector.memset(alpha_column[:], 0.0)
         all_ones = keep.tile([P, P], BF16)
         nc.vector.memset(all_ones[:], 1.0)
+        warm_rows = keep.tile([P, WARM_COLS], F32)
+        nc.gpsimd.memset(warm_rows[:], 0.0)
         table_loader = keep.tile([P, 1], BF16)
         nc.scalar.activation(out=table_loader[:], in_=ones[:], func=ACT.Abs)
 
@@ -151,6 +154,10 @@ def tile_ternarylinear_s_kernel(tc, x, weight, alpha, bias, out):
         turned[3] = turn_in_order(nc, psum_turn, w_sb[:, 3, :], ident[:])
         nc.tensor.matmul(
             out=delta[:, 1:2], lhsT=all_ones[:], rhs=alpha_column[:], start=True, stop=True
+        )
+        warm = psum_turn.tile([P, WORDS], F32, tag="turned")
+        nc.tensor.matmul(
+            out=warm[:], lhsT=mean_weights[:], rhs=warm_rows[:], start=True, stop=True
         )
         half_alpha = keep.tile([P, 1], F32)
         abs_on_vector(1, whole)

@@ -305,13 +305,13 @@ def tile_ternarylinear_s_kernel(tc, x, weight, alpha, bias, out):
         quantise(tiles(6))
         multiply(6, bank_56, 1)
         times_alpha(tiles(7))
+        add_bias_and_store(bank_34, 3, 2)
         quantise(tiles(2))
         bank_2 = new_bank()
         multiply(2, bank_2, 0)
         quantise(tiles(7))
         bank_7 = new_bank()
         multiply(7, bank_7, 0)
-        add_bias_and_store(bank_34, 3, 2)
         add_bias_and_store(bank_56, 5, 2)
         add_bias_and_store(bank_2, 2, 1)
         add_bias_and_store(bank_7, 7, 1)

@@ -300,18 +300,26 @@ def tile_ternarylinear_s_kernel(tc, x, weight, alpha, bias, out):
         quantise(tiles(5))
         bank_56 = new_bank()
         multiply(5, bank_56, 0)
+        warm_again = new_bank()
+        nc.tensor.matmul(
+            out=warm_again[:, : 2 * P],
+            lhsT=mean_weights[:],
+            rhs=warm_rows[:, : 2 * P],
+            start=True,
+            stop=True,
+        )
         times_alpha(tiles(6))
         to_ternary(tiles(7))
         quantise(tiles(6))
         multiply(6, bank_56, 1)
         times_alpha(tiles(7))
         add_bias_and_store(bank_34, 3, 2)
-        quantise(tiles(2))
-        bank_2 = new_bank()
-        multiply(2, bank_2, 0)
         quantise(tiles(7))
         bank_7 = new_bank()
         multiply(7, bank_7, 0)
+        quantise(tiles(2))
+        bank_2 = new_bank()
+        multiply(2, bank_2, 0)
         add_bias_and_store(bank_56, 5, 2)
-        add_bias_and_store(bank_2, 2, 1)
         add_bias_and_store(bank_7, 7, 1)
+        add_bias_and_store(bank_2, 2, 1)

from contextlib import ExitStack

import concourse.mybir as mybir
from concourse.masks import make_identity

BF16 = mybir.dt.bfloat16
F32 = mybir.dt.float32
I32 = mybir.dt.int32
U32 = mybir.dt.uint32
U8 = mybir.dt.uint8
FP8X4 = mybir.dt.float8_e4m3fn_x4
ALU = mybir.AluOpType
ACT = mybir.ActivationFunctionType

P = 128
D_IN = 1024
D_OUT = 1024
O_TILES = D_OUT // P
K_PASS = 4 * P
PASSES = D_IN // K_PASS
WORDS = D_IN // 2
TURNS = WORDS // P
CODE_COLS = PASSES * P
BANK_COLS = 512
MAGNITUDE_BITS = 0x7FFF7FFF
TERNARY_BITS = -0x3FFF4000
EDGE = (2.0 - 2.0**-8) * (1.0 - 2.0**-22)
WARM_COLS = 512
SUM_COLS = 16

FLOPS = 2 * P * D_IN * D_OUT


def turn(nc, psum, rows_bf16, ident):
    words = rows_bf16.bitcast(F32)
    turned = psum.tile([P, TURNS, P], F32, tag="turned")
    for j in range(TURNS):
        nc.tensor.transpose(turned[:, j, :], words[:, j * P : (j + 1) * P], ident)
    return turned


def copy_grouped(nc, turned, grouped):
    nc.scalar.copy(
        out=grouped.bitcast(F32).rearrange("p (g r u) -> p g r u", g=PASSES, u=2),
        in_=turned[:].rearrange("p (g u) r -> p g r u", u=2),
    )


def turn_in_order(nc, psum, rows_bf16, ident):
    words = rows_bf16.bitcast(F32)
    turned = psum.tile([P, WORDS], F32, tag="turned")
    by_word = turned[:].rearrange("p (g r u) -> p g r u", g=PASSES, u=2)
    for g in range(PASSES):
        for u in range(2):
            j = 2 * g + u
            nc.tensor.transpose(by_word[:, g, :, u], words[:, j * P : (j + 1) * P], ident)
    return turned


def tile_ternarylinear_s_kernel(tc, x, weight, alpha, bias, out):
    nc = tc.nc
    x_rows = x.flatten_outer_dims()
    out_rows = out.flatten_outer_dims()
    w_tiles = weight.rearrange("(t p) d -> t p d", p=P)

    with ExitStack() as ctx:
        ctx.enter_context(tc.manual_schedule())
        keep = ctx.enter_context(tc.tile_pool(name="keep", bufs=1))
        work = ctx.enter_context(tc.tile_pool(name="work", bufs=3))
        psum_turn = ctx.enter_context(tc.psum_pool(name="psum_turn", bufs=7))
        psum_sum = ctx.enter_context(tc.psum_pool(name="psum_sum", bufs=1))

        ident = keep.tile([P, P], F32)
        make_identity(nc, ident[:])
        mean_weights = keep.tile([P, P], F32)
        nc.vector.memset(mean_weights[:], 0.7 / (D_OUT * D_IN) / EDGE)
        partial = keep.tile([P, SUM_COLS], F32)
        nc.vector.memset(partial[:], 2.0**-100)
        delta = psum_sum.tile([P, BANK_COLS], F32, tag="delta")
        ones = keep.tile([P, 1], BF16)
        nc.vector.memset(ones[:], 1.0)
        alpha_column = keep.tile([P, 1], BF16)
        nc.vector.memset(alpha_column[:], 0.0)
        all_ones = keep.tile([P, P], BF16)
        nc.vector.memset(all_ones[:], 1.0)
        warm_rows = keep.tile([P, WARM_COLS], F32)
        nc.gpsimd.memset(warm_rows[:], 0.0)
        table_loader = keep.tile([P, 1], BF16)
        nc.scalar.activation(out=table_loader[:], in_=ones[:], func=ACT.Abs)

        w_sb = keep.tile([P, O_TILES, D_IN], BF16)
        for t in range(O_TILES):
            nc.sync.dma_start(out=w_sb[:, t, :], in_=w_tiles[t])
        nc.scalar.dma_start(out=alpha_column[0:1, :], in_=alpha.partition_broadcast(1))
        x_sb = keep.tile([P, D_IN], BF16)
        nc.sync.dma_start(out=x_sb[:], in_=x_rows)
        bias_sb = keep.tile([P, D_OUT], BF16)
        nc.sync.dma_start(out=bias_sb[:], in_=bias.partition_broadcast(P))

        magnitude = keep.tile([P, O_TILES, D_IN], BF16)
        w_grouped = keep.tile([P, O_TILES, D_IN], BF16, align_bytes=64)

        def abs_on_vector(t, cols):
            nc.vector.tensor_scalar(
                out=magnitude[:, t, cols].bitcast(I32),
                in0=w_sb[:, t, cols].bitcast(I32),
                scalar1=MAGNITUDE_BITS,
                scalar2=None,
                op0=ALU.bitwise_and,
            )

        def sum_on_scalar(t, cols, sum_col):
            nc.scalar.activation(
                out=magnitude[:, t, cols],
                in_=w_sb[:, t, cols],
                func=ACT.Abs,
                accum_out=partial[:, sum_col : sum_col + 1],
            )

        def sum_on_vector(t, cols, sum_col, initial=None):
            unused = work.tile([P, D_IN], BF16, tag="unused")
            nc.vector.tensor_scalar(
                out=unused[:, cols],
                in0=magnitude[:, t, cols],
                scalar1=1.0,
                scalar2=initial,
                op0=ALU.mult,
                op1=ALU.add,
                accum_out=partial[:, sum_col : sum_col + 1],
            )

        turned = {}

        def copy_turned(t):
            copy_grouped(nc, turned[t], w_grouped[:, t, :])

        whole = slice(0, D_IN)
        first_half = slice(0, D_IN // 2)
        second_half = slice(D_IN // 2, D_IN)
        def add_to_delta(col, first=False, last=False):
            nc.tensor.matmul(
                out=delta[:, 0:1],
                lhsT=mean_weights[:],
                rhs=partial[:, col : col + 1],
                start=first,
                stop=last,
            )

        for t, col in ((0, 0), (2, 1), (4, 5), (6, 6)):
            sum_on_scalar(t, whole, col)
        for t in (0, 1, 2):
            turned[t] = turn(nc, psum_turn, w_sb[:, t, :], ident[:])
            copy_turned(t)
        turned[3] = turn_in_order(nc, psum_turn, w_sb[:, 3, :], ident[:])
        nc.tensor.matmul(
            out=delta[:, 1:2], lhsT=all_ones[:], rhs=alpha_column[:], start=True, stop=True
        )
        warm = psum_turn.tile([P, WORDS], F32, tag="turned")
        nc.tensor.matmul(
            out=warm[:], lhsT=mean_weights[:], rhs=warm_rows[:], start=True, stop=True
        )
        half_alpha = keep.tile([P, 1], F32)
        abs_on_vector(1, whole)
        sum_on_vector(1, whole, 4)
        abs_on_vector(3, whole)
        sum_on_vector(3, whole, 2, initial=partial[:, 4:5])
        abs_on_vector(5, whole)
        nc.vector.reduce_sum(out=partial[:, 8:9], in_=partial[:, 0:4], axis=mybir.AxisListType.X)
        nc.vector.tensor_scalar(
            out=half_alpha[:], in0=delta[:, 1:2], scalar1=0.5, scalar2=None, op0=ALU.mult
        )
        sum_on_vector(5, whole, 7, initial=partial[:, 8:9])
        abs_on_vector(7, whole)
        sum_on_vector(7, whole, 9, initial=partial[:, 7:8])
        add_to_delta(5, first=True)
        add_to_delta(6)
        add_to_delta(9, last=True)
        turned_x = turn(nc, psum_turn, x_sb[:], ident[:])
        for t in (4, 5, 6, 7):
            turned[t] = turn_in_order(nc, psum_turn, w_sb[:, t, :], ident[:])
        x_grouped = keep.tile([P, D_IN], BF16, align_bytes=64)
        to_edge = keep.tile([P, 1], F32)
        nc.vector.reciprocal(out=to_edge[:], in_=delta[:, 0:1])

        scaled = keep.tile([P, O_TILES, D_IN], BF16, align_bytes=64)
        ternary = keep.tile([P, O_TILES, D_IN], BF16, align_bytes=64)
        w_q = keep.tile([P, O_TILES, D_IN], BF16, align_bytes=64)

        def scale_on_vector(t):
            nc.vector.tensor_scalar(
                out=scaled[:, t, :],
                in0=w_grouped[:, t, :],
                scalar1=to_edge[:, 0:1],
                scalar2=None,
                op0=ALU.mult,
            )

        def scale_on_scalar(t):
            nc.scalar.activation(
                out=scaled[:, t, :],
                in_=turned[t][:].bitcast(BF16),
                func=ACT.Copy,
                scale=to_edge[:, 0:1],
            )

        def tiles(first, count=1):
            return slice(first, first + count)

        def to_ternary(ts):
            nc.vector.tensor_scalar(
                out=ternary[:, ts, :].bitcast(I32),
                in0=scaled[:, ts, :].bitcast(I32),
                scalar1=TERNARY_BITS,
                scalar2=None,
                op0=ALU.bitwise_and,
            )

        def times_alpha(ts):
            nc.vector.tensor_scalar(
                out=w_q[:, ts, :],
                in0=ternary[:, ts, :],
                scalar1=half_alpha[:, 0:1],
                scalar2=None,
                op0=ALU.mult,
            )

        def times_alpha_on_scalar(t):
            nc.scalar.activation(
                out=w_q[:, t, :], in_=ternary[:, t, :], func=ACT.Copy, scale=half_alpha[:, 0:1]
            )

        x_codes = keep.tile([P, CODE_COLS], U32, align_bytes=64)
        x_scales = keep.tile([P, CODE_COLS], U8, align_bytes=64)
        w_codes = keep.tile([P, O_TILES, CODE_COLS], U32, align_bytes=64)
        w_scales = keep.tile([P, O_TILES, CODE_COLS], U8, align_bytes=64)
        out_sb = keep.tile([P, D_OUT], F32)

        def quantise(ts):
            nc.vector.quantize_mx(
                out=w_codes[:, ts, :].rearrange("p t c -> p (t c)").bitcast(FP8X4),
                scales=w_scales[:, ts, :].rearrange("p t c -> p (t c)"),
                in_=w_q[:, ts, :].rearrange("p t d -> p (t d)"),
            )

        def new_bank():
            return psum_turn.tile([P, WORDS], F32, tag="turned", name="products")

        def multiply(t, bank, place):
            for g in range(PASSES):
                cols = slice(g * P, (g + 1) * P)
                nc.tensor.matmul_mx(
                    out=bank[:, place * P : (place + 1) * P],
                    lhsT=x_codes[:, cols].bitcast(FP8X4),
                    lhsT_scale=x_scales[:, cols],
                    rhs=w_codes[:, t, cols].bitcast(FP8X4),
                    rhs_scale=w_scales[:, t, cols],
                    start=(g == 0),
                    stop=(g == PASSES - 1),
                )

        def add_bias_and_store(bank, first_tile, count):
            o_cols = slice(first_tile * P, (first_tile + count) * P)
            nc.vector.tensor_tensor(
                out=out_sb[:, o_cols],
                in0=bank[:, : count * P],
                in1=bias_sb[:, o_cols],
                op=ALU.add,
            )
            nc.sync.dma_start(out=out_rows[:, o_cols], in_=out_sb[:, o_cols])

        scale_on_scalar(3)
        copy_grouped(nc, turned_x, x_grouped[:])
        for t in range(4, O_TILES):
            scale_on_scalar(t)

        for t in (0, 1, 2):
            scale_on_vector(t)
        to_ternary(tiles(0, 2))
        to_ternary(tiles(2))
        times_alpha_on_scalar(2)
        times_alpha(tiles(0, 2))
        to_ternary(tiles(3))
        nc.vector.quantize_mx(out=x_codes[:].bitcast(FP8X4), scales=x_scales[:], in_=x_grouped[:])
        times_alpha(tiles(3))
        quantise(tiles(0, 2))
        bank_01 = new_bank()
        multiply(0, bank_01, 0)
        multiply(1, bank_01, 1)
        to_ternary(tiles(4))
        quantise(tiles(3))
        bank_34 = new_bank()
        multiply(3, bank_34, 0)
        times_alpha(tiles(4))
        to_ternary(tiles(5))
        add_bias_and_store(bank_01, 0, 2)
        quantise(tiles(4))
        multiply(4, bank_34, 1)
        times_alpha(tiles(5))
        to_ternary(tiles(6))
        quantise(tiles(5))
        bank_56 = new_bank()
        multiply(5, bank_56, 0)
        warm_again = new_bank()
        nc.tensor.matmul(
            out=warm_again[:, : 2 * P],
            lhsT=mean_weights[:],
            rhs=warm_rows[:, : 2 * P],
            start=True,
            stop=True,
        )
        times_alpha(tiles(6))
        to_ternary(tiles(7))
        quantise(tiles(6))
        multiply(6, bank_56, 1)
        times_alpha(tiles(7))
        add_bias_and_store(bank_34, 3, 2)
        quantise(tiles(7))
        bank_7 = new_bank()
        multiply(7, bank_7, 0)
        quantise(tiles(2))
        bank_2 = new_bank()
        multiply(2, bank_2, 0)
        add_bias_and_store(bank_56, 5, 2)
        add_bias_and_store(bank_7, 7, 1)
        add_bias_and_store(bank_2, 2, 1)
